import numpy as np
import ml_dtypes


def mxq(x, axis, fmt="e4m3"):
    dtype, down = {"e4m3": (ml_dtypes.float8_e4m3fn, 7), "e5m2": (ml_dtypes.float8_e5m2, 14)}[fmt]
    v = np.moveaxis(np.asarray(x, np.float32).astype(ml_dtypes.bfloat16).astype(np.float64), axis, -1)
    blocks = v.reshape(v.shape[:-1] + (-1, 32))
    amax = np.abs(blocks).max(-1, keepdims=True)
    byte = np.maximum(np.where(amax > 0, np.frexp(amax)[1] - 1 + 127, 0) - down, 1)
    scale = np.exp2(byte - 127.0)
    codes = (blocks / scale).astype(np.float32).astype(dtype).astype(np.float64)
    return np.moveaxis((codes * scale).reshape(v.shape), -1, axis)


WIDE = False


def mx_kscale(k):
    if not WIDE:
        return np.ones(k)
    levels = np.array([10, -10, 5, -5, 0])
    a = np.random.permutation(np.resize(levels, k // 512 * 4)).reshape(k // 512, 4)
    idx = np.arange(k)
    return np.exp2(a[idx // 512, idx % 128 // 32])


BF16 = ml_dtypes.bfloat16


def bf(x):
    return np.asarray(x, np.float32).astype(BF16)


def f64(x):
    return np.asarray(x).astype(np.float64)


B, N_VAR, D = 128, 8, 512
NUM_UNITS = N_VAR * D


def sigmoid(v):
    return 1.0 / (1.0 + np.exp(-v))


def setup_inputs():
    s = mx_kscale(D)
    return {
        "inputs": bf(np.random.standard_normal((B, N_VAR))),
        "hidden": bf((np.random.standard_normal((B, D, N_VAR)) * s[None, :, None]).reshape(B, NUM_UNITS)),
        "gate_w_I2H": bf(np.random.standard_normal((N_VAR, 1, 2 * D, 1)) * 0.5),
        "gate_w_H2H": bf(np.random.standard_normal((N_VAR, 1, 2 * D, D)) / np.sqrt(D) / s),
        "gate_bias": bf(np.random.standard_normal(2 * NUM_UNITS) * 0.4),
        "update_w_I2H": bf(np.random.standard_normal((N_VAR, 1, D, 1)) * 0.5),
        "update_w_H2H": bf(np.random.standard_normal((N_VAR, 1, D, D)) * 1.5 / np.sqrt(D) / s),
        "update_bias": bf(np.random.standard_normal(NUM_UNITS) * 0.4),
    }


def reference(inputs, hidden, gate_w_I2H, gate_w_H2H, gate_bias, update_w_I2H, update_w_H2H, update_bias):
    inputs, hidden = f64(inputs), f64(hidden)
    b, num_units = hidden.shape
    n_var = inputs.shape[1]
    d = num_units // n_var

    x_v = inputs.T
    h_v = hidden.reshape(b, d, n_var).transpose(2, 0, 1)

    gx = x_v[:, :, None] * f64(gate_w_I2H)[:, 0, :, 0][:, None, :]
    gh = mxq(h_v, 2, "e4m3") @ mxq(f64(gate_w_H2H)[:, 0], 2, "e4m3").transpose(0, 2, 1)
    res_gate = (gx + gh).transpose(1, 0, 2).reshape(b, 2 * num_units) + f64(gate_bias)
    z, r = res_gate[:, :num_units], res_gate[:, num_units:]

    r_v = sigmoid(r).reshape(b, d, n_var).transpose(2, 0, 1)

    ux = x_v[:, :, None] * f64(update_w_I2H)[:, 0, :, 0][:, None, :]
    uh = mxq(h_v * r_v, 2, "e4m3") @ mxq(f64(update_w_H2H)[:, 0], 2, "e4m3").transpose(0, 2, 1)
    g = (ux + uh).transpose(1, 0, 2).reshape(b, num_units) + f64(update_bias)

    zs = sigmoid(z)
    return zs * hidden + (1.0 - zs) * np.tanh(g)

@@ -1,0 +1,238 @@
+from contextlib import ExitStack
+
+import concourse.mybir as mybir
+from concourse.masks import make_identity
+
+F32 = mybir.dt.float32
+BF16 = mybir.dt.bfloat16
+U32 = mybir.dt.uint32
+U8 = mybir.dt.uint8
+I32 = mybir.dt.int32
+FP8X4 = mybir.dt.float8_e4m3fn_x4
+ALU = mybir.AluOpType
+ACTF = mybir.ActivationFunctionType
+
+P = 128
+FLOPS = 2 * 128 * 512 * (8192 + 4096)
+
+N_CHUNKS = 24
+
+
+def tile_grucell_kernel(
+    tc, x_in, hidden, gate_w_i2h, gate_w_h2h, gate_bias, update_w_i2h, update_w_h2h, update_bias, out
+):
+    nc = tc.nc
+    gw = gate_w_h2h.rearrange("v o c j -> (v o c) j")
+    uw = update_w_h2h.rearrange("v o c j -> (v o c) j")
+    gwi = gate_w_i2h.rearrange("v o c i -> (v o c i)")
+    uwi = update_w_i2h.rearrange("v o c i -> (v o c i)")
+
+    with ExitStack() as ctx:
+        const = ctx.enter_context(tc.tile_pool(name="const", bufs=1))
+        rawp = ctx.enter_context(tc.tile_pool(name="rawp", bufs=6))
+        grpp = ctx.enter_context(tc.tile_pool(name="grpp", bufs=3))
+        codp = ctx.enter_context(tc.tile_pool(name="codp", bufs=3))
+        wrk = ctx.enter_context(tc.tile_pool(name="wrk", bufs=3))
+        ps_w = ctx.enter_context(tc.psum_pool(name="ps_w", bufs=4))
+        ps_a = ctx.enter_context(tc.psum_pool(name="ps_a", bufs=2))
+        ps_b = ctx.enter_context(tc.psum_pool(name="ps_b", bufs=2))
+
+        x_sb = const.tile([P, 8], BF16, name="x_sb")
+        nc.scalar.dma_start(out=x_sb[:], in_=x_in)
+        sv = const.tile([P, 6, 32], BF16, name="sv")
+        nc.scalar.dma_start(out=sv[:, 0, :].rearrange("p (u n) -> p u n", u=2),
+                            in_=gwi[4096:8192].rearrange("(u p n) -> p u n", u=2, n=16))
+        nc.scalar.dma_start(out=sv[:, 1, :].rearrange("p (u n) -> p u n", u=2),
+                            in_=gate_bias[4096:8192].rearrange("(u p n) -> p u n", u=2, n=16))
+
+        hid = const.tile([P, 4096], BF16, name="hid")
+        for half in range(2):
+            nc.sync.dma_start(out=hid[:, 2048 * half:2048 * half + 2048],
+                              in_=hidden[:, 2048 * half:2048 * half + 2048])
+
+        raws = []
+        for pr in range(12):
+            raw = rawp.tile([P, 8, 512], BF16, name="raw")
+            if pr < 4:
+                u, h = pr // 2, pr % 2
+                src = gw[4096 + 2048 * u:4096 + 2048 * u + 2048, :].rearrange("(p n) j -> p n j", n=16)
+                nc.sync.dma_start(out=raw[:], in_=src[:, 8 * h:8 * h + 8, :])
+            else:
+                mat = gw if pr < 8 else uw
+                m = (pr - 4) % 4
+                src = mat[1024 * m:1024 * m + 1024, :].rearrange("(s p n) j -> p s n j", s=2, n=4)
+                nc.sync.dma_start(out=raw[:].rearrange("p (s n) j -> p s n j", s=2), in_=src)
+            raws.append(raw)
+            if pr == 1:
+                for idx, vecsrc in ((2, gwi[0:4096]), (3, gate_bias[0:4096]), (4, uwi), (5, update_bias)):
+                    nc.scalar.dma_start(out=sv[:, idx, :].rearrange("p (s n) -> p s n", s=8),
+                                        in_=vecsrc.rearrange("(s p n) -> p s n", s=8, n=4))
+
+        ident_f = const.tile([P, P], F32, name="ident_f")
+        make_identity(nc, ident_f[:])
+        ident_b = const.tile([P, P], BF16, name="ident_b")
+        make_identity(nc, ident_b[:])
+
+        warm = const.tile([P, 1], F32, name="warm")
+        nc.vector.memset(warm[:], 0.0)
+        nc.scalar.activation(out=warm[:], in_=warm[:], func=ACTF.Sigmoid)
+
+        rcodes = []
+        rscales = []
+        for i in range(2):
+            rc = const.tile([P, 768], U32, name="rcodes%d" % i, align_bytes=64)
+            rs_ = const.tile([P, 768], U8, name="rscales%d" % i, align_bytes=64)
+            nc.vector.memset(rc[:].bitcast(I32), 0)
+            nc.vector.memset(rs_[:].bitcast(I32), 0)
+            rcodes.append(rc)
+            rscales.append(rs_)
+
+        xrep = const.tile([P, 4, 64], BF16, name="xrep")
+        nc.vector.tensor_copy(out=xrep[:], in_=x_sb[:, 4:8].unsqueeze(2).to_broadcast([P, 4, 64]))
+        xb = const.tile([P, 10, P], F32, name="xb")
+        for g in range(2):
+            xp = ps_a.tile([P, 4, P], F32, name="acc")
+            for vi in range(4):
+                v = 4 * g + vi
+                nc.tensor.matmul(out=xp[:, vi, :], lhsT=x_sb[:, v:v + 1].to_broadcast([P, P]), rhs=ident_b[:],
+                                 start=True, stop=True)
+            nc.vector.tensor_copy(out=xb[:, 4 * g:4 * g + 4, :], in_=xp[:])
+        xp2 = ps_b.tile([P, 4, P], F32, name="bk")
+        for u in range(2):
+            nc.tensor.matmul(out=xp2[:, u, :], lhsT=xrep[:, 2 * u:2 * u + 2, :].rearrange("p a c -> p (a c)"),
+                             rhs=ident_b[:], start=True, stop=True)
+        nc.vector.tensor_copy(out=xb[:, 8:10, :], in_=xp2[:, 0:2, :])
+
+        svf = const.tile([P, 6, 32], F32, name="svf")
+        nc.vector.tensor_copy(out=svf[:, 0:2, :], in_=sv[:, 0:2, :])
+        nc.vector.tensor_copy(out=svf[:, 2:6, :], in_=sv[:, 2:6, :])
+
+        hs = const.tile([P, 8, 512], BF16, name="hs")
+        for half in range(2):
+            src = hid[:, 2048 * half:2048 * half + 2048].rearrange("b (j v) -> b v j", v=8)
+            nc.vector.tensor_copy(out=hs[:, 0:5, 256 * half:256 * half + 256], in_=src[:, 0:5, :])
+            nc.scalar.copy(out=hs[:, 5:8, 256 * half:256 * half + 256], in_=src[:, 5:8, :])
+        hgrp = const.tile([P, 8, P, 2], F32, name="hgrp", align_bytes=64)
+        for vp in range(4):
+            ht = ps_w.tile([P, 2, 2, P], F32, name="wt")
+            for vi in range(2):
+                for uk in range(2):
+                    nc.tensor.transpose(ht[:, vi, uk, :],
+                                        hs[:, 2 * vp + vi, :].bitcast(F32)[:, 128 * uk:128 * uk + 128], ident_f[:])
+            eng_copy = nc.scalar.copy if vp % 2 == 0 else nc.vector.tensor_copy
+            eng_copy(out=hgrp[:, 2 * vp:2 * vp + 2, :, :], in_=ht[:].rearrange("p v u b -> p v b u"))
+        hq = const.tile([P, 1024], U32, name="hq", align_bytes=64)
+        hqs = const.tile([P, 1024], U8, name="hqs", align_bytes=64)
+        nc.vector.quantize_mx(out=hq[:].bitcast(FP8X4), scales=hqs[:],
+                              in_=hgrp[:].rearrange("p v b u -> p (v b u)").bitcast(BF16))
+
+        rs_all = const.tile([P, 4, 8, P], F32, name="rs_all")
+        zs_t = const.tile([P, 8, 4, P], F32, name="zs_t")
+        a_nat = const.tile([P, 8, 512], F32, name="a_nat")
+        hrg = const.tile([P, 8, P, 4], BF16, name="hrg", align_bytes=64)
+        hrq = const.tile([P, 1024], U32, name="hrq", align_bytes=64)
+        hrqs = const.tile([P, 1024], U8, name="hrqs", align_bytes=64)
+
+        for k in range(N_CHUNKS):
+            kind = k // 8
+            s = k % 8
+            raw = raws[k // 2]
+            wts = []
+            for hb in range(2):
+                wt = ps_w.tile([P, 2, 2, P], F32, name="wt")
+                for bi in range(2):
+                    for uk in range(2):
+                        nc.tensor.transpose(
+                            wt[:, bi, uk, :],
+                            raw[:, 4 * (k % 2) + 2 * hb + bi, :].bitcast(F32)[:, 128 * uk:128 * uk + 128],
+                            ident_f[:])
+                wts.append(wt)
+            grp = grpp.tile([P, 4, P, 2], F32, name="grp", align_bytes=64)
+            for hb in range(2):
+                nc.scalar.copy(out=grp[:, 2 * hb:2 * hb + 2, :, :], in_=wts[hb][:].rearrange("p i u c -> p i c u"))
+
+            acc = ps_a.tile([P, 4, P], F32, name="acc")
+            if kind == 0:
+                u = s // 4
+                codes, scales = rcodes[k % 2], rscales[k % 2]
+                for i in range(4):
+                    for h in range(2):
+                        c0 = 192 * i + 128 * h
+                        nc.vector.quantize_mx(
+                            out=codes[:, c0:c0 + 64].bitcast(FP8X4), scales=scales[:, c0:c0 + 64],
+                            in_=grp[:, i, 64 * h:64 * h + 64, :].rearrange("p c u -> p (c u)").bitcast(BF16))
+                for i in range(4):
+                    for h in range(2):
+                        c0 = 192 * i + 64 * h
+                        v = 4 + 2 * u + h
+                        nc.tensor.matmul_mx(
+                            out=acc[:, i, :],
+                            lhsT=codes[:, c0:c0 + 128].bitcast(FP8X4), lhsT_scale=scales[:, c0:c0 + 128],
+                            rhs=hq[:, 128 * v:128 * v + 128].bitcast(FP8X4), rhs_scale=hqs[:, 128 * v:128 * v + 128],
+                            start=(h == 0), stop=(h == 1))
+            else:
+                codes = codp.tile([P, 512], U32, name="codes", align_bytes=64)
+                scales = codp.tile([P, 512], U8, name="scales", align_bytes=64)
+                nc.vector.quantize_mx(out=codes[:].bitcast(FP8X4), scales=scales[:],
+                                      in_=grp[:].rearrange("p i c u -> p (i c u)").bitcast(BF16))
+                if kind == 1:
+                    v = s // 2
+                    mov, movs = hq, hqs
+                else:
+                    v = s
+                    mov, movs = hrq, hrqs
+                for i in range(4):
+                    nc.tensor.matmul_mx(
+                        out=acc[:, i, :],
+                        lhsT=codes[:, 128 * i:128 * i + 128].bitcast(FP8X4), lhsT_scale=scales[:, 128 * i:128 * i + 128],
+                        rhs=mov[:, 128 * v:128 * v + 128].bitcast(FP8X4), rhs_scale=movs[:, 128 * v:128 * v + 128],
+                        start=True, stop=True)
+
+            tmp = wrk.tile([P, 4, P], F32, name="tmp")
+            if kind == 2:
+                tg = wrk.tile([P, 4, P], F32, name="tg")
+            for i in range(4):
+                if kind == 0:
+                    n = 4 * (s % 4) + i
+                    xcol = 8 + s // 4
+                    col = 16 * (s // 4) + n
+                    dst = rs_all[:, 2 * (s // 4) + n // 8, n % 8, :]
+                else:
+                    xcol = s // 2 if kind == 1 else s
+                    col = 4 * s + i
+                    dst = zs_t[:, s, i, :] if kind == 1 else tg[:, i, :]
+                nc.vector.scalar_tensor_tensor(out=tmp[:, i, :], in0=xb[:, xcol, :], scalar=svf[:, 2 * kind, col:col + 1],
+                                               in1=acc[:, i, :], op0=ALU.mult, op1=ALU.add)
+                nc.scalar.activation(out=dst, in_=tmp[:, i, :], func=(ACTF.Tanh if kind == 2 else ACTF.Sigmoid),
+                                     bias=svf[:, 2 * kind + 1, col:col + 1], scale=1.0)
+
+            if k == 7:
+                hgb = hgrp[:].rearrange("p v b u -> p v (b u)").bitcast(BF16).rearrange("p v (b t) -> p v b t", t=4)
+                for v in range(8):
+                    nc.vector.tensor_tensor(out=hrg[:, v, :, :], in0=rs_all[:, :, v, :].rearrange("p t b -> p b t"),
+                                            in1=hgb[:, v, :, :], op=ALU.mult)
+                nc.vector.quantize_mx(out=hrq[:].bitcast(FP8X4), scales=hrqs[:],
+                                      in_=hrg[:].rearrange("p v b t -> p (v b t)"))
+
+            if kind == 1:
+                bk = ps_b.tile([P, 4, P], F32, name="bk")
+                for i in range(4):
+                    nc.tensor.transpose(bk[:, i, :], zs_t[:, s, i, :], ident_f[:])
+                nc.vector.tensor_tensor(out=a_nat[:, s, :].rearrange("b (p n) -> b p n", n=4),
+                                        in0=bk[:].rearrange("b n p -> b p n"),
+                                        in1=hid[:, 512 * s:512 * s + 512].rearrange("b (p n) -> b p n", n=4),
+                                        op=ALU.mult)
+            if kind == 2:
+                nt = wrk.tile([P, 4, P], F32, name="nt")
+                nc.vector.scalar_tensor_tensor(out=nt[:].rearrange("p n b -> p (n b)"),
+                                               in0=zs_t[:, s, :, :].rearrange("p n b -> p (n b)"), scalar=1.0,
+                                               in1=tg[:].rearrange("p n b -> p (n b)"),
+                                               op0=ALU.subtract, op1=ALU.mult)
+                bk = ps_b.tile([P, 4, P], F32, name="bk")
+                for i in range(4):
+                    nc.tensor.transpose(bk[:, i, :], nt[:, i, :], ident_f[:])
+                o_sb = wrk.tile([P, 512], F32, name="o_sb")
+                nc.vector.tensor_tensor(out=o_sb[:].rearrange("b (p n) -> b p n", n=4),
+                                        in0=a_nat[:, s, :].rearrange("b (p n) -> b p n", n=4),
+                                        in1=bk[:].rearrange("b n p -> b p n"), op=ALU.subtract)
+                nc.sync.dma_start(out=out[:, 512 * s:512 * s + 512], in_=o_sb[:])

@@ -14,8 +14,14 @@ ACTF = mybir.ActivationFunctionType
 
 P = 128
 FLOPS = 2 * 128 * 512 * (8192 + 4096)
-
 N_CHUNKS = 24
+
+MANUAL = True
+HR_POOL = True
+N_POOL_UPTO = 7
+DVE_EVAC = ((1, 1), (3, 1), (5, 1), (7, 1))
+RAW_BUFS = 8
+QH_STEPS = (13, 18)
 
 
 def tile_grucell_kernel(
@@ -29,13 +35,16 @@ def tile_grucell_kernel(
 
     with ExitStack() as ctx:
         const = ctx.enter_context(tc.tile_pool(name="const", bufs=1))
-        rawp = ctx.enter_context(tc.tile_pool(name="rawp", bufs=6))
+        rawp = ctx.enter_context(tc.tile_pool(name="rawp", bufs=RAW_BUFS))
         grpp = ctx.enter_context(tc.tile_pool(name="grpp", bufs=3))
         codp = ctx.enter_context(tc.tile_pool(name="codp", bufs=3))
         wrk = ctx.enter_context(tc.tile_pool(name="wrk", bufs=3))
+        wrk4 = ctx.enter_context(tc.tile_pool(name="wrk4", bufs=4))
         ps_w = ctx.enter_context(tc.psum_pool(name="ps_w", bufs=4))
         ps_a = ctx.enter_context(tc.psum_pool(name="ps_a", bufs=2))
         ps_b = ctx.enter_context(tc.psum_pool(name="ps_b", bufs=2))
+        if MANUAL:
+            ctx.enter_context(tc.manual_schedule())
 
         x_sb = const.tile([P, 8], BF16, name="x_sb")
         nc.scalar.dma_start(out=x_sb[:], in_=x_in)
@@ -54,24 +63,24 @@ def tile_grucell_kernel(
         for pr in range(12):
             raw = rawp.tile([P, 8, 512], BF16, name="raw")
             if pr < 4:
-                u, h = pr // 2, pr % 2
-                src = gw[4096 + 2048 * u:4096 + 2048 * u + 2048, :].rearrange("(p n) j -> p n j", n=16)
-                nc.sync.dma_start(out=raw[:], in_=src[:, 8 * h:8 * h + 8, :])
+                u, vh = pr % 2, pr // 2
+                src = gw[4096 + 2048 * u:4096 + 2048 * u + 2048, :].rearrange(
+                    "(p e w i) j -> p e w i j", e=2, w=2, i=4)
+                nc.sync.dma_start(out=raw[:].rearrange("p (e i) j -> p e i j", e=2), in_=src[:, :, vh, :, :])
             else:
                 mat = gw if pr < 8 else uw
                 m = (pr - 4) % 4
                 src = mat[1024 * m:1024 * m + 1024, :].rearrange("(s p n) j -> p s n j", s=2, n=4)
                 nc.sync.dma_start(out=raw[:].rearrange("p (s n) j -> p s n j", s=2), in_=src)
             raws.append(raw)
-            if pr == 1:
-                for idx, vecsrc in ((2, gwi[0:4096]), (3, gate_bias[0:4096]), (4, uwi), (5, update_bias)):
-                    nc.scalar.dma_start(out=sv[:, idx, :].rearrange("p (s n) -> p s n", s=8),
-                                        in_=vecsrc.rearrange("(s p n) -> p s n", s=8, n=4))
 
-        ident_f = const.tile([P, P], F32, name="ident_f")
-        make_identity(nc, ident_f[:])
         ident_b = const.tile([P, P], BF16, name="ident_b")
         make_identity(nc, ident_b[:])
+        ident_f = const.tile([P, P], F32, name="ident_f")
+        make_identity(nc, ident_f[:])
+        for idx, vecsrc in ((2, gwi[0:4096]), (3, gate_bias[0:4096]), (4, uwi), (5, update_bias)):
+            nc.gpsimd.dma_start(out=sv[:, idx, :].rearrange("p (s n) -> p s n", s=8),
+                                in_=vecsrc.rearrange("(s p n) -> p s n", s=8, n=4))
 
         warm = const.tile([P, 1], F32, name="warm")
         nc.vector.memset(warm[:], 0.0)
@@ -90,6 +99,11 @@ def tile_grucell_kernel(
         xrep = const.tile([P, 4, 64], BF16, name="xrep")
         nc.vector.tensor_copy(out=xrep[:], in_=x_sb[:, 4:8].unsqueeze(2).to_broadcast([P, 4, 64]))
         xb = const.tile([P, 10, P], F32, name="xb")
+        xp2 = ps_b.tile([P, 4, P], F32, name="bk")
+        for u in range(2):
+            nc.tensor.matmul(out=xp2[:, u, :], lhsT=xrep[:, 2 * u:2 * u + 2, :].rearrange("p a c -> p (a c)"),
+                             rhs=ident_b[:], start=True, stop=True)
+        nc.vector.tensor_copy(out=xb[:, 8:10, :], in_=xp2[:, 0:2, :])
         for g in range(2):
             xp = ps_a.tile([P, 4, P], F32, name="acc")
             for vi in range(4):
@@ -97,15 +111,9 @@ def tile_grucell_kernel(
                 nc.tensor.matmul(out=xp[:, vi, :], lhsT=x_sb[:, v:v + 1].to_broadcast([P, P]), rhs=ident_b[:],
                                  start=True, stop=True)
             nc.vector.tensor_copy(out=xb[:, 4 * g:4 * g + 4, :], in_=xp[:])
-        xp2 = ps_b.tile([P, 4, P], F32, name="bk")
-        for u in range(2):
-            nc.tensor.matmul(out=xp2[:, u, :], lhsT=xrep[:, 2 * u:2 * u + 2, :].rearrange("p a c -> p (a c)"),
-                             rhs=ident_b[:], start=True, stop=True)
-        nc.vector.tensor_copy(out=xb[:, 8:10, :], in_=xp2[:, 0:2, :])
 
         svf = const.tile([P, 6, 32], F32, name="svf")
         nc.vector.tensor_copy(out=svf[:, 0:2, :], in_=sv[:, 0:2, :])
-        nc.vector.tensor_copy(out=svf[:, 2:6, :], in_=sv[:, 2:6, :])
 
         hs = const.tile([P, 8, 512], BF16, name="hs")
         for half in range(2):
@@ -113,7 +121,7 @@ def tile_grucell_kernel(
             nc.vector.tensor_copy(out=hs[:, 0:5, 256 * half:256 * half + 256], in_=src[:, 0:5, :])
             nc.scalar.copy(out=hs[:, 5:8, 256 * half:256 * half + 256], in_=src[:, 5:8, :])
         hgrp = const.tile([P, 8, P, 2], F32, name="hgrp", align_bytes=64)
-        for vp in range(4):
+        for vp in (2, 3, 0, 1):
             ht = ps_w.tile([P, 2, 2, P], F32, name="wt")
             for vi in range(2):
                 for uk in range(2):
@@ -123,21 +131,22 @@ def tile_grucell_kernel(
             eng_copy(out=hgrp[:, 2 * vp:2 * vp + 2, :, :], in_=ht[:].rearrange("p v u b -> p v b u"))
         hq = const.tile([P, 1024], U32, name="hq", align_bytes=64)
         hqs = const.tile([P, 1024], U8, name="hqs", align_bytes=64)
-        nc.vector.quantize_mx(out=hq[:].bitcast(FP8X4), scales=hqs[:],
-                              in_=hgrp[:].rearrange("p v b u -> p (v b u)").bitcast(BF16))
+        for hh in (1, 0):
+            nc.vector.quantize_mx(out=hq[:, 512 * hh:512 * hh + 512].bitcast(FP8X4), scales=hqs[:, 512 * hh:512 * hh + 512],
+                                  in_=hgrp[:, 4 * hh:4 * hh + 4, :, :].rearrange("p v b u -> p (v b u)").bitcast(BF16))
+        hgb = hgrp[:].rearrange("p v b u -> p v (b u)").bitcast(BF16).rearrange("p v (b t) -> p v b t", t=4)
 
         rs_all = const.tile([P, 4, 8, P], F32, name="rs_all")
-        zs_t = const.tile([P, 8, 4, P], F32, name="zs_t")
-        a_nat = const.tile([P, 8, 512], F32, name="a_nat")
+        q_t = const.tile([P, 8, 4, P], F32, name="q_t")
+        nega = const.tile([P, 8, 512], F32, name="nega")
         hrg = const.tile([P, 8, P, 4], BF16, name="hrg", align_bytes=64)
         hrq = const.tile([P, 1024], U32, name="hrq", align_bytes=64)
         hrqs = const.tile([P, 1024], U8, name="hrqs", align_bytes=64)
 
-        for k in range(N_CHUNKS):
-            kind = k // 8
-            s = k % 8
+        st = {}
+
+        def do_t(k):
             raw = raws[k // 2]
-            wts = []
             for hb in range(2):
                 wt = ps_w.tile([P, 2, 2, P], F32, name="wt")
                 for bi in range(2):
@@ -146,14 +155,18 @@ def tile_grucell_kernel(
                             wt[:, bi, uk, :],
                             raw[:, 4 * (k % 2) + 2 * hb + bi, :].bitcast(F32)[:, 128 * uk:128 * uk + 128],
                             ident_f[:])
-                wts.append(wt)
-            grp = grpp.tile([P, 4, P, 2], F32, name="grp", align_bytes=64)
-            for hb in range(2):
-                nc.scalar.copy(out=grp[:, 2 * hb:2 * hb + 2, :, :], in_=wts[hb][:].rearrange("p i u c -> p i c u"))
+                st[("wt", k, hb)] = wt
 
-            acc = ps_a.tile([P, 4, P], F32, name="acc")
-            if kind == 0:
-                u = s // 4
+        def do_c(k):
+            grp = grpp.tile([P, 4, P, 2], F32, name="grp", align_bytes=64)
+            st[("grp", k)] = grp
+            for hb in range(2):
+                eng_copy = nc.vector.tensor_copy if (k, hb) in DVE_EVAC else nc.scalar.copy
+                eng_copy(out=grp[:, 2 * hb:2 * hb + 2, :, :], in_=st[("wt", k, hb)][:].rearrange("p i u c -> p i c u"))
+
+        def do_q(k):
+            grp = st[("grp", k)]
+            if k < 8:
                 codes, scales = rcodes[k % 2], rscales[k % 2]
                 for i in range(4):
                     for h in range(2):
@@ -161,6 +174,20 @@ def tile_grucell_kernel(
                         nc.vector.quantize_mx(
                             out=codes[:, c0:c0 + 64].bitcast(FP8X4), scales=scales[:, c0:c0 + 64],
                             in_=grp[:, i, 64 * h:64 * h + 64, :].rearrange("p c u -> p (c u)").bitcast(BF16))
+            else:
+                codes = codp.tile([P, 512], U32, name="codes", align_bytes=64)
+                scales = codp.tile([P, 512], U8, name="scales", align_bytes=64)
+                nc.vector.quantize_mx(out=codes[:].bitcast(FP8X4), scales=scales[:],
+                                      in_=grp[:].rearrange("p i c u -> p (i c u)").bitcast(BF16))
+            st[("codes", k)] = (codes, scales)
+
+        def do_m(k):
+            codes, scales = st[("codes", k)]
+            acc = ps_a.tile([P, 4, P], F32, name="acc")
+            st[("acc", k)] = acc
+            s = k % 8
+            if k < 8:
+                u = (k // 2) % 2
                 for i in range(4):
                     for h in range(2):
                         c0 = 192 * i + 64 * h
@@ -171,16 +198,8 @@ def tile_grucell_kernel(
                             rhs=hq[:, 128 * v:128 * v + 128].bitcast(FP8X4), rhs_scale=hqs[:, 128 * v:128 * v + 128],
                             start=(h == 0), stop=(h == 1))
             else:
-                codes = codp.tile([P, 512], U32, name="codes", align_bytes=64)
-                scales = codp.tile([P, 512], U8, name="scales", align_bytes=64)
-                nc.vector.quantize_mx(out=codes[:].bitcast(FP8X4), scales=scales[:],
-                                      in_=grp[:].rearrange("p i c u -> p (i c u)").bitcast(BF16))
-                if kind == 1:
-                    v = s // 2
-                    mov, movs = hq, hqs
-                else:
-                    v = s
-                    mov, movs = hrq, hrqs
+                v = s // 2 if k < 16 else s
+                mov, movs = (hq, hqs) if k < 16 else (hrq, hrqs)
                 for i in range(4):
                     nc.tensor.matmul_mx(
                         out=acc[:, i, :],
@@ -188,51 +207,96 @@ def tile_grucell_kernel(
                         rhs=mov[:, 128 * v:128 * v + 128].bitcast(FP8X4), rhs_scale=movs[:, 128 * v:128 * v + 128],
                         start=True, stop=True)
 
+        def do_sa(k):
+            kind, s = k // 8, k % 8
+            acc = st[("acc", k)]
             tmp = wrk.tile([P, 4, P], F32, name="tmp")
             if kind == 2:
-                tg = wrk.tile([P, 4, P], F32, name="tg")
+                tg = wrk4.tile([P, 4, P], F32, name="tg")
+                st[("tg", k)] = tg
             for i in range(4):
                 if kind == 0:
-                    n = 4 * (s % 4) + i
-                    xcol = 8 + s // 4
-                    col = 16 * (s // 4) + n
-                    dst = rs_all[:, 2 * (s // 4) + n // 8, n % 8, :]
+                    u, vh, e = (k // 2) % 2, k // 4, k % 2
+                    xcol = 8 + u
+                    col = 16 * u + 8 * e + 4 * vh + i
+                    dst = rs_all[:, 2 * u + e, 4 * vh + i, :]
                 else:
                     xcol = s // 2 if kind == 1 else s
                     col = 4 * s + i
-                    dst = zs_t[:, s, i, :] if kind == 1 else tg[:, i, :]
+                    dst = q_t[:, s, i, :] if kind == 1 else tg[:, i, :]
                 nc.vector.scalar_tensor_tensor(out=tmp[:, i, :], in0=xb[:, xcol, :], scalar=svf[:, 2 * kind, col:col + 1],
                                                in1=acc[:, i, :], op0=ALU.mult, op1=ALU.add)
                 nc.scalar.activation(out=dst, in_=tmp[:, i, :], func=(ACTF.Tanh if kind == 2 else ACTF.Sigmoid),
-                                     bias=svf[:, 2 * kind + 1, col:col + 1], scale=1.0)
+                                     bias=svf[:, 2 * kind + 1, col:col + 1], scale=(-1.0 if kind == 1 else 1.0))
 
-            if k == 7:
-                hgb = hgrp[:].rearrange("p v b u -> p v (b u)").bitcast(BF16).rearrange("p v (b t) -> p v b t", t=4)
-                for v in range(8):
-                    nc.vector.tensor_tensor(out=hrg[:, v, :, :], in0=rs_all[:, :, v, :].rearrange("p t b -> p b t"),
-                                            in1=hgb[:, v, :, :], op=ALU.mult)
-                nc.vector.quantize_mx(out=hrq[:].bitcast(FP8X4), scales=hrqs[:],
-                                      in_=hrg[:].rearrange("p v b t -> p (v b t)"))
+        def do_hr(v):
+            eng = nc.gpsimd if HR_POOL else nc.vector
+            eng.tensor_tensor(out=hrg[:, v, :, :], in0=rs_all[:, :, v, :].rearrange("p t b -> p b t"),
+                              in1=hgb[:, v, :, :], op=ALU.mult)
 
-            if kind == 1:
-                bk = ps_b.tile([P, 4, P], F32, name="bk")
-                for i in range(4):
-                    nc.tensor.transpose(bk[:, i, :], zs_t[:, s, i, :], ident_f[:])
-                nc.vector.tensor_tensor(out=a_nat[:, s, :].rearrange("b (p n) -> b p n", n=4),
-                                        in0=bk[:].rearrange("b n p -> b p n"),
-                                        in1=hid[:, 512 * s:512 * s + 512].rearrange("b (p n) -> b p n", n=4),
-                                        op=ALU.mult)
-            if kind == 2:
-                nt = wrk.tile([P, 4, P], F32, name="nt")
-                nc.vector.scalar_tensor_tensor(out=nt[:].rearrange("p n b -> p (n b)"),
-                                               in0=zs_t[:, s, :, :].rearrange("p n b -> p (n b)"), scalar=1.0,
-                                               in1=tg[:].rearrange("p n b -> p (n b)"),
+        def do_qh(hh):
+            nc.vector.quantize_mx(out=hrq[:, 512 * hh:512 * hh + 512].bitcast(FP8X4),
+                                  scales=hrqs[:, 512 * hh:512 * hh + 512],
+                                  in_=hrg[:, 4 * hh:4 * hh + 4, :, :].rearrange("p v b t -> p (v b t)"))
+
+        def do_n(k):
+            s = k % 8
+            nt = wrk4.tile([P, 4, P], F32, name="nt")
+            st[("nt", k)] = nt
+            eng = nc.gpsimd if s < N_POOL_UPTO else nc.vector
+            eng.tensor_tensor(out=nt[:].rearrange("p n b -> p (n b)"), in0=q_t[:, s, :, :].rearrange("p n b -> p (n b)"),
+                              in1=st[("tg", k)][:].rearrange("p n b -> p (n b)"), op=ALU.mult)
+
+        def do_b(k):
+            s = k % 8
+            bk = ps_b.tile([P, 4, P], F32, name="bk")
+            st[("bk", k)] = bk
+            for i in range(4):
+                nc.tensor.transpose(bk[:, i, :], q_t[:, s, i, :] if k < 16 else st[("nt", k)][:, i, :], ident_f[:])
+
+        def do_x(k):
+            s = k % 8
+            bkv = st[("bk", k)][:].rearrange("b n p -> b p n")
+            if k < 16:
+                nc.vector.scalar_tensor_tensor(out=nega[:, s, :].rearrange("b (p n) -> b p n", n=4), in0=bkv, scalar=1.0,
+                                               in1=hid[:, 512 * s:512 * s + 512].rearrange("b (p n) -> b p n", n=4),
                                                op0=ALU.subtract, op1=ALU.mult)
-                bk = ps_b.tile([P, 4, P], F32, name="bk")
-                for i in range(4):
-                    nc.tensor.transpose(bk[:, i, :], nt[:, i, :], ident_f[:])
+            else:
                 o_sb = wrk.tile([P, 512], F32, name="o_sb")
-                nc.vector.tensor_tensor(out=o_sb[:].rearrange("b (p n) -> b p n", n=4),
-                                        in0=a_nat[:, s, :].rearrange("b (p n) -> b p n", n=4),
-                                        in1=bk[:].rearrange("b n p -> b p n"), op=ALU.subtract)
+                nc.vector.tensor_tensor(out=o_sb[:].rearrange("b (p n) -> b p n", n=4), in0=bkv,
+                                        in1=nega[:, s, :].rearrange("b (p n) -> b p n", n=4), op=ALU.subtract)
                 nc.sync.dma_start(out=out[:, 512 * s:512 * s + 512], in_=o_sb[:])
+
+        def step_b(k):
+            if k < 16:
+                return k + 2
+            return k + 3 if (k % 8) < N_POOL_UPTO else k + 2 + 0
+
+        for i in range(N_CHUNKS + 6):
+            if i < N_CHUNKS:
+                do_t(i)
+            for k in range(8, N_CHUNKS):
+                if step_b(k) == i:
+                    do_b(k)
+            if 1 <= i <= N_CHUNKS:
+                do_q(i - 1)
+                do_m(i - 1)
+            if i == 6:
+                nc.vector.tensor_copy(out=svf[:, 2, :], in_=sv[:, 2, :])
+                nc.vector.tensor_scalar_mul(out=svf[:, 3, :], in0=sv[:, 3, :], scalar1=-1.0)
+                nc.vector.tensor_copy(out=svf[:, 4:6, :], in_=sv[:, 4:6, :])
+            for hh in range(2):
+                if i == QH_STEPS[hh]:
+                    do_qh(hh)
+            for k in range(8, N_CHUNKS):
+                if step_b(k) + 1 == i:
+                    do_x(k)
+            if i < N_CHUNKS:
+                do_c(i)
+            if 1 <= i <= N_CHUNKS:
+                do_sa(i - 1)
+                if i - 1 == 3 or i - 1 == 7:
+                    for v in range(i - 4, i):
+                        do_hr(v)
+                if i - 1 >= 16:
+                    do_n(i - 1)

@@ -22,6 +22,10 @@ N_POOL_UPTO = 7
 DVE_EVAC = ((1, 1), (3, 1), (5, 1), (7, 1))
 RAW_BUFS = 8
 QH_STEPS = (13, 18)
+WARM1 = 4
+WARM2 = 6
+D_STEP0 = 2
+D_STEP = 1
 
 
 def tile_grucell_kernel(
@@ -86,6 +90,22 @@ def tile_grucell_kernel(
         nc.vector.memset(warm[:], 0.0)
         nc.scalar.activation(out=warm[:], in_=warm[:], func=ACTF.Sigmoid)
 
+        zc = const.tile([P, 512], U32, name="zc", align_bytes=64)
+        zsc = const.tile([P, 512], U8, name="zsc", align_bytes=64)
+        zsrc = const.tile([P, 2048], BF16, name="zsrc", align_bytes=64)
+        nc.vector.memset(zsrc[:].bitcast(I32), 0)
+        nc.vector.quantize_mx(out=zc[:].bitcast(FP8X4), scales=zsc[:], in_=zsrc[:])
+
+        def dummies(bank, count):
+            for d in range(count):
+                nc.tensor.matmul_mx(out=bank[:].rearrange("p a b -> p (a b)"),
+                                    lhsT=zc[:, 0:128].bitcast(FP8X4), lhsT_scale=zsc[:, 0:128],
+                                    rhs=zc[:].bitcast(FP8X4), rhs_scale=zsc[:], start=True, stop=True)
+
+        if WARM1 > 0:
+            wbank = ps_a.tile([P, 4, P], F32, name="acc")
+            dummies(wbank, WARM1)
+
         rcodes = []
         rscales = []
         for i in range(2):
@@ -111,6 +131,10 @@ def tile_grucell_kernel(
                 nc.tensor.matmul(out=xp[:, vi, :], lhsT=x_sb[:, v:v + 1].to_broadcast([P, P]), rhs=ident_b[:],
                                  start=True, stop=True)
             nc.vector.tensor_copy(out=xb[:, 4 * g:4 * g + 4, :], in_=xp[:])
+
+        if WARM2 > 0:
+            wbank = ps_a.tile([P, 4, P], F32, name="acc")
+            dummies(wbank, WARM2)
 
         svf = const.tile([P, 6, 32], F32, name="svf")
         nc.vector.tensor_copy(out=svf[:, 0:2, :], in_=sv[:, 0:2, :])
@@ -185,6 +209,7 @@ def tile_grucell_kernel(
             codes, scales = st[("codes", k)]
             acc = ps_a.tile([P, 4, P], F32, name="acc")
             st[("acc", k)] = acc
+            dummies(acc, D_STEP)
             s = k % 8
             if k < 8:
                 u = (k // 2) % 2
@@ -275,6 +300,9 @@ def tile_grucell_kernel(
         for i in range(N_CHUNKS + 6):
             if i < N_CHUNKS:
                 do_t(i)
+            if i == 0 and D_STEP0 > 0:
+                wbank = ps_a.tile([P, 4, P], F32, name="acc")
+                dummies(wbank, D_STEP0)
             for k in range(8, N_CHUNKS):
                 if step_b(k) == i:
                     do_b(k)

@@ -18,14 +18,18 @@ N_CHUNKS = 24
 
 MANUAL = True
 HR_POOL = True
-N_POOL_UPTO = 7
+N_POOL_UPTO = 6
 DVE_EVAC = ((1, 1), (3, 1), (5, 1), (7, 1))
 RAW_BUFS = 8
-QH_STEPS = (13, 18)
-WARM1 = 4
-WARM2 = 6
-D_STEP0 = 2
-D_STEP = 1
+QH_STEPS = (12, 17)
+WARM1 = 0
+WARM2 = 0
+D_STEP0 = 0
+D_STEP = 0
+LAG_M = 2
+LAG_BZ = 4
+LAG_BG = 5
+N_RCODES = 3
 
 
 def tile_grucell_kernel(
@@ -90,11 +94,12 @@ def tile_grucell_kernel(
         nc.vector.memset(warm[:], 0.0)
         nc.scalar.activation(out=warm[:], in_=warm[:], func=ACTF.Sigmoid)
 
-        zc = const.tile([P, 512], U32, name="zc", align_bytes=64)
-        zsc = const.tile([P, 512], U8, name="zsc", align_bytes=64)
-        zsrc = const.tile([P, 2048], BF16, name="zsrc", align_bytes=64)
-        nc.vector.memset(zsrc[:].bitcast(I32), 0)
-        nc.vector.quantize_mx(out=zc[:].bitcast(FP8X4), scales=zsc[:], in_=zsrc[:])
+        if WARM1 + WARM2 + D_STEP0 + D_STEP > 0:
+            zc = const.tile([P, 512], U32, name="zc", align_bytes=64)
+            zsc = const.tile([P, 512], U8, name="zsc", align_bytes=64)
+            zsrc = const.tile([P, 2048], BF16, name="zsrc", align_bytes=64)
+            nc.vector.memset(zsrc[:].bitcast(I32), 0)
+            nc.vector.quantize_mx(out=zc[:].bitcast(FP8X4), scales=zsc[:], in_=zsrc[:])
 
         def dummies(bank, count):
             for d in range(count):
@@ -108,7 +113,7 @@ def tile_grucell_kernel(
 
         rcodes = []
         rscales = []
-        for i in range(2):
+        for i in range(N_RCODES):
             rc = const.tile([P, 768], U32, name="rcodes%d" % i, align_bytes=64)
             rs_ = const.tile([P, 768], U8, name="rscales%d" % i, align_bytes=64)
             nc.vector.memset(rc[:].bitcast(I32), 0)
@@ -191,7 +196,7 @@ def tile_grucell_kernel(
         def do_q(k):
             grp = st[("grp", k)]
             if k < 8:
-                codes, scales = rcodes[k % 2], rscales[k % 2]
+                codes, scales = rcodes[k % N_RCODES], rscales[k % N_RCODES]
                 for i in range(4):
                     for h in range(2):
                         c0 = 192 * i + 128 * h
@@ -292,12 +297,15 @@ def tile_grucell_kernel(
                                         in1=nega[:, s, :].rearrange("b (p n) -> b p n", n=4), op=ALU.subtract)
                 nc.sync.dma_start(out=out[:, 512 * s:512 * s + 512], in_=o_sb[:])
 
+        def n_on_pool(k):
+            return (k % 8) < N_POOL_UPTO
+
         def step_b(k):
             if k < 16:
-                return k + 2
-            return k + 3 if (k % 8) < N_POOL_UPTO else k + 2 + 0
+                return k + LAG_BZ
+            return k + LAG_BG if n_on_pool(k) else k + LAG_M + 2
 
-        for i in range(N_CHUNKS + 6):
+        for i in range(N_CHUNKS + 10):
             if i < N_CHUNKS:
                 do_t(i)
             if i == 0 and D_STEP0 > 0:
@@ -306,9 +314,11 @@ def tile_grucell_kernel(
             for k in range(8, N_CHUNKS):
                 if step_b(k) == i:
                     do_b(k)
-            if 1 <= i <= N_CHUNKS:
+            if 0 <= i - 1 < N_CHUNKS:
                 do_q(i - 1)
-                do_m(i - 1)
+            km = i - LAG_M
+            if 0 <= km < N_CHUNKS:
+                do_m(km)
             if i == 6:
                 nc.vector.tensor_copy(out=svf[:, 2, :], in_=sv[:, 2, :])
                 nc.vector.tensor_scalar_mul(out=svf[:, 3, :], in0=sv[:, 3, :], scalar1=-1.0)
@@ -316,15 +326,17 @@ def tile_grucell_kernel(
             for hh in range(2):
                 if i == QH_STEPS[hh]:
                     do_qh(hh)
+            if 16 <= km - 1 < N_CHUNKS and not n_on_pool(km - 1):
+                do_n(km - 1)
             for k in range(8, N_CHUNKS):
                 if step_b(k) + 1 == i:
                     do_x(k)
             if i < N_CHUNKS:
                 do_c(i)
-            if 1 <= i <= N_CHUNKS:
-                do_sa(i - 1)
-                if i - 1 == 3 or i - 1 == 7:
-                    for v in range(i - 4, i):
+            if 0 <= km < N_CHUNKS:
+                do_sa(km)
+                if km == 3 or km == 7:
+                    for v in range(km - 3, km + 1):
                         do_hr(v)
-                if i - 1 >= 16:
-                    do_n(i - 1)
+                if km >= 16 and n_on_pool(km):
+                    do_n(km)

@@ -22,10 +22,12 @@ N_POOL_UPTO = 6
 DVE_EVAC = ((1, 1), (3, 1), (5, 1), (7, 1))
 RAW_BUFS = 8
 QH_STEPS = (12, 17)
-WARM1 = 0
-WARM2 = 0
-D_STEP0 = 0
-D_STEP = 0
+WARM1 = 6
+WARM2 = 12
+D_STEP0 = 3
+D_STEP = 1
+D_STEP_ZG = 2
+D_HT = 2
 LAG_M = 2
 LAG_BZ = 4
 LAG_BG = 5
@@ -94,7 +96,7 @@ def tile_grucell_kernel(
         nc.vector.memset(warm[:], 0.0)
         nc.scalar.activation(out=warm[:], in_=warm[:], func=ACTF.Sigmoid)
 
-        if WARM1 + WARM2 + D_STEP0 + D_STEP > 0:
+        if True:
             zc = const.tile([P, 512], U32, name="zc", align_bytes=64)
             zsc = const.tile([P, 512], U8, name="zsc", align_bytes=64)
             zsrc = const.tile([P, 2048], BF16, name="zsrc", align_bytes=64)
@@ -107,9 +109,8 @@ def tile_grucell_kernel(
                                     lhsT=zc[:, 0:128].bitcast(FP8X4), lhsT_scale=zsc[:, 0:128],
                                     rhs=zc[:].bitcast(FP8X4), rhs_scale=zsc[:], start=True, stop=True)
 
-        if WARM1 > 0:
-            wbank = ps_a.tile([P, 4, P], F32, name="acc")
-            dummies(wbank, WARM1)
+        wbank = ps_b.tile([P, 4, P], F32, name="bk")
+        dummies(wbank, WARM1)
 
         rcodes = []
         rscales = []
@@ -137,9 +138,7 @@ def tile_grucell_kernel(
                                  start=True, stop=True)
             nc.vector.tensor_copy(out=xb[:, 4 * g:4 * g + 4, :], in_=xp[:])
 
-        if WARM2 > 0:
-            wbank = ps_a.tile([P, 4, P], F32, name="acc")
-            dummies(wbank, WARM2)
+        dummies(wbank, WARM2)
 
         svf = const.tile([P, 6, 32], F32, name="svf")
         nc.vector.tensor_copy(out=svf[:, 0:2, :], in_=sv[:, 0:2, :])
@@ -158,6 +157,8 @@ def tile_grucell_kernel(
                                         hs[:, 2 * vp + vi, :].bitcast(F32)[:, 128 * uk:128 * uk + 128], ident_f[:])
             eng_copy = nc.scalar.copy if vp % 2 == 0 else nc.vector.tensor_copy
             eng_copy(out=hgrp[:, 2 * vp:2 * vp + 2, :, :], in_=ht[:].rearrange("p v u b -> p v b u"))
+            if vp % 2 == 1:
+                dummies(wbank, D_HT)
         hq = const.tile([P, 1024], U32, name="hq", align_bytes=64)
         hqs = const.tile([P, 1024], U8, name="hqs", align_bytes=64)
         for hh in (1, 0):
@@ -214,7 +215,7 @@ def tile_grucell_kernel(
             codes, scales = st[("codes", k)]
             acc = ps_a.tile([P, 4, P], F32, name="acc")
             st[("acc", k)] = acc
-            dummies(acc, D_STEP)
+            dummies(acc, D_STEP if k < 8 else D_STEP_ZG)
             s = k % 8
             if k < 8:
                 u = (k // 2) % 2
@@ -308,8 +309,7 @@ def tile_grucell_kernel(
         for i in range(N_CHUNKS + 10):
             if i < N_CHUNKS:
                 do_t(i)
-            if i == 0 and D_STEP0 > 0:
-                wbank = ps_a.tile([P, 4, P], F32, name="acc")
+            if i < LAG_M:
                 dummies(wbank, D_STEP0)
             for k in range(8, N_CHUNKS):
                 if step_b(k) == i:

@@ -20,17 +20,13 @@ MANUAL = True
 HR_POOL = True
 N_POOL_UPTO = 6
 DVE_EVAC = ((1, 1), (3, 1), (5, 1), (7, 1))
-RAW_BUFS = 8
-QH_STEPS = (12, 17)
-WARM1 = 6
-WARM2 = 12
-D_STEP0 = 3
-D_STEP = 1
-D_STEP_ZG = 2
-D_HT = 2
+RAW_BUFS = 16
+QH_STEPS = (13, 18)
+LAG_S = 2
+LAG_A = 3
 LAG_M = 2
-LAG_BZ = 4
-LAG_BG = 5
+LAG_BZ = 5
+LAG_BG = 6
 N_RCODES = 3
 
 
@@ -70,47 +66,31 @@ def tile_grucell_kernel(
                               in_=hidden[:, 2048 * half:2048 * half + 2048])
 
         raws = []
-        for pr in range(12):
-            raw = rawp.tile([P, 8, 512], BF16, name="raw")
-            if pr < 4:
-                u, vh = pr % 2, pr // 2
+        for k in range(N_CHUNKS):
+            raw = rawp.tile([P, 4, 512], BF16, name="raw")
+            if k < 8:
+                u, vh, e = (k // 2) % 2, k // 4, k % 2
                 src = gw[4096 + 2048 * u:4096 + 2048 * u + 2048, :].rearrange(
                     "(p e w i) j -> p e w i j", e=2, w=2, i=4)
-                nc.sync.dma_start(out=raw[:].rearrange("p (e i) j -> p e i j", e=2), in_=src[:, :, vh, :, :])
+                nc.sync.dma_start(out=raw[:], in_=src[:, e, vh, :, :])
             else:
-                mat = gw if pr < 8 else uw
-                m = (pr - 4) % 4
-                src = mat[1024 * m:1024 * m + 1024, :].rearrange("(s p n) j -> p s n j", s=2, n=4)
-                nc.sync.dma_start(out=raw[:].rearrange("p (s n) j -> p s n j", s=2), in_=src)
+                mat = gw if k < 16 else uw
+                s = k % 8
+                nc.sync.dma_start(out=raw[:], in_=mat[512 * s:512 * s + 512, :].rearrange("(p n) j -> p n j", n=4))
             raws.append(raw)
+            if k == 5:
+                for idx, vecsrc in ((2, gwi[0:4096]), (3, gate_bias[0:4096]), (4, uwi), (5, update_bias)):
+                    nc.sync.dma_start(out=sv[:, idx, :].rearrange("p (s n) -> p s n", s=8),
+                                      in_=vecsrc.rearrange("(s p n) -> p s n", s=8, n=4))
 
         ident_b = const.tile([P, P], BF16, name="ident_b")
         make_identity(nc, ident_b[:])
         ident_f = const.tile([P, P], F32, name="ident_f")
         make_identity(nc, ident_f[:])
-        for idx, vecsrc in ((2, gwi[0:4096]), (3, gate_bias[0:4096]), (4, uwi), (5, update_bias)):
-            nc.gpsimd.dma_start(out=sv[:, idx, :].rearrange("p (s n) -> p s n", s=8),
-                                in_=vecsrc.rearrange("(s p n) -> p s n", s=8, n=4))
 
         warm = const.tile([P, 1], F32, name="warm")
         nc.vector.memset(warm[:], 0.0)
         nc.scalar.activation(out=warm[:], in_=warm[:], func=ACTF.Sigmoid)
-
-        if True:
-            zc = const.tile([P, 512], U32, name="zc", align_bytes=64)
-            zsc = const.tile([P, 512], U8, name="zsc", align_bytes=64)
-            zsrc = const.tile([P, 2048], BF16, name="zsrc", align_bytes=64)
-            nc.vector.memset(zsrc[:].bitcast(I32), 0)
-            nc.vector.quantize_mx(out=zc[:].bitcast(FP8X4), scales=zsc[:], in_=zsrc[:])
-
-        def dummies(bank, count):
-            for d in range(count):
-                nc.tensor.matmul_mx(out=bank[:].rearrange("p a b -> p (a b)"),
-                                    lhsT=zc[:, 0:128].bitcast(FP8X4), lhsT_scale=zsc[:, 0:128],
-                                    rhs=zc[:].bitcast(FP8X4), rhs_scale=zsc[:], start=True, stop=True)
-
-        wbank = ps_b.tile([P, 4, P], F32, name="bk")
-        dummies(wbank, WARM1)
 
         rcodes = []
         rscales = []
@@ -129,16 +109,19 @@ def tile_grucell_kernel(
         for u in range(2):
             nc.tensor.matmul(out=xp2[:, u, :], lhsT=xrep[:, 2 * u:2 * u + 2, :].rearrange("p a c -> p (a c)"),
                              rhs=ident_b[:], start=True, stop=True)
-        nc.vector.tensor_copy(out=xb[:, 8:10, :], in_=xp2[:, 0:2, :])
+        xps = []
         for g in range(2):
             xp = ps_a.tile([P, 4, P], F32, name="acc")
             for vi in range(4):
                 v = 4 * g + vi
                 nc.tensor.matmul(out=xp[:, vi, :], lhsT=x_sb[:, v:v + 1].to_broadcast([P, P]), rhs=ident_b[:],
                                  start=True, stop=True)
-            nc.vector.tensor_copy(out=xb[:, 4 * g:4 * g + 4, :], in_=xp[:])
+            xps.append(xp)
 
-        dummies(wbank, WARM2)
+        def do_xev():
+            nc.scalar.copy(out=xb[:, 8:10, :], in_=xp2[:, 0:2, :])
+            for g in range(2):
+                nc.scalar.copy(out=xb[:, 4 * g:4 * g + 4, :], in_=xps[g][:])
 
         svf = const.tile([P, 6, 32], F32, name="svf")
         nc.vector.tensor_copy(out=svf[:, 0:2, :], in_=sv[:, 0:2, :])
@@ -146,24 +129,28 @@ def tile_grucell_kernel(
         hs = const.tile([P, 8, 512], BF16, name="hs")
         for half in range(2):
             src = hid[:, 2048 * half:2048 * half + 2048].rearrange("b (j v) -> b v j", v=8)
-            nc.vector.tensor_copy(out=hs[:, 0:5, 256 * half:256 * half + 256], in_=src[:, 0:5, :])
-            nc.scalar.copy(out=hs[:, 5:8, 256 * half:256 * half + 256], in_=src[:, 5:8, :])
+            cols = slice(256 * half, 256 * half + 256)
+            nc.vector.tensor_copy(out=hs[:, 0:4, cols], in_=src[:, 0:4, :])
+            nc.scalar.copy(out=hs[:, 4:6, cols], in_=src[:, 4:6, :])
+            nc.gpsimd.tensor_scalar(out=hs[:, 6:8, cols], in0=src[:, 6:8, :], scalar1=1.0, scalar2=0.0,
+                                    op0=ALU.mult, op1=ALU.add)
         hgrp = const.tile([P, 8, P, 2], F32, name="hgrp", align_bytes=64)
-        for vp in (2, 3, 0, 1):
-            ht = ps_w.tile([P, 2, 2, P], F32, name="wt")
-            for vi in range(2):
-                for uk in range(2):
-                    nc.tensor.transpose(ht[:, vi, uk, :],
-                                        hs[:, 2 * vp + vi, :].bitcast(F32)[:, 128 * uk:128 * uk + 128], ident_f[:])
-            eng_copy = nc.scalar.copy if vp % 2 == 0 else nc.vector.tensor_copy
-            eng_copy(out=hgrp[:, 2 * vp:2 * vp + 2, :, :], in_=ht[:].rearrange("p v u b -> p v b u"))
-            if vp % 2 == 1:
-                dummies(wbank, D_HT)
         hq = const.tile([P, 1024], U32, name="hq", align_bytes=64)
         hqs = const.tile([P, 1024], U8, name="hqs", align_bytes=64)
-        for hh in (1, 0):
+
+        def do_h(hh):
+            for vp in (2 * hh, 2 * hh + 1):
+                ht = ps_w.tile([P, 2, 2, P], F32, name="wt")
+                for vi in range(2):
+                    for uk in range(2):
+                        nc.tensor.transpose(ht[:, vi, uk, :],
+                                            hs[:, 2 * vp + vi, :].bitcast(F32)[:, 128 * uk:128 * uk + 128], ident_f[:])
+                eng_copy = nc.scalar.copy if vp % 2 == 0 else nc.vector.tensor_copy
+                eng_copy(out=hgrp[:, 2 * vp:2 * vp + 2, :, :], in_=ht[:].rearrange("p v u b -> p v b u"))
             nc.vector.quantize_mx(out=hq[:, 512 * hh:512 * hh + 512].bitcast(FP8X4), scales=hqs[:, 512 * hh:512 * hh + 512],
                                   in_=hgrp[:, 4 * hh:4 * hh + 4, :, :].rearrange("p v b u -> p (v b u)").bitcast(BF16))
+
+        do_h(1)
         hgb = hgrp[:].rearrange("p v b u -> p v (b u)").bitcast(BF16).rearrange("p v (b t) -> p v b t", t=4)
 
         rs_all = const.tile([P, 4, 8, P], F32, name="rs_all")
@@ -176,14 +163,14 @@ def tile_grucell_kernel(
         st = {}
 
         def do_t(k):
-            raw = raws[k // 2]
+            raw = raws[k]
             for hb in range(2):
                 wt = ps_w.tile([P, 2, 2, P], F32, name="wt")
                 for bi in range(2):
                     for uk in range(2):
                         nc.tensor.transpose(
                             wt[:, bi, uk, :],
-                            raw[:, 4 * (k % 2) + 2 * hb + bi, :].bitcast(F32)[:, 128 * uk:128 * uk + 128],
+                            raw[:, 2 * hb + bi, :].bitcast(F32)[:, 128 * uk:128 * uk + 128],
                             ident_f[:])
                 st[("wt", k, hb)] = wt
 
@@ -215,7 +202,6 @@ def tile_grucell_kernel(
             codes, scales = st[("codes", k)]
             acc = ps_a.tile([P, 4, P], F32, name="acc")
             st[("acc", k)] = acc
-            dummies(acc, D_STEP if k < 8 else D_STEP_ZG)
             s = k % 8
             if k < 8:
                 u = (k // 2) % 2
@@ -238,25 +224,36 @@ def tile_grucell_kernel(
                         rhs=mov[:, 128 * v:128 * v + 128].bitcast(FP8X4), rhs_scale=movs[:, 128 * v:128 * v + 128],
                         start=True, stop=True)
 
-        def do_sa(k):
+        def block_args(k, i):
             kind, s = k // 8, k % 8
+            if kind == 0:
+                u, vh, e = (k // 2) % 2, k // 4, k % 2
+                return 8 + u, 16 * u + 8 * e + 4 * vh + i
+            return (s // 2 if kind == 1 else s), 4 * s + i
+
+        def do_s(k):
             acc = st[("acc", k)]
             tmp = wrk.tile([P, 4, P], F32, name="tmp")
+            st[("tmp", k)] = tmp
+            for i in range(4):
+                xcol, col = block_args(k, i)
+                nc.vector.scalar_tensor_tensor(out=tmp[:, i, :], in0=xb[:, xcol, :],
+                                               scalar=svf[:, 2 * (k // 8), col:col + 1],
+                                               in1=acc[:, i, :], op0=ALU.mult, op1=ALU.add)
+
+        def do_a(k):
+            kind, s = k // 8, k % 8
+            tmp = st[("tmp", k)]
             if kind == 2:
                 tg = wrk4.tile([P, 4, P], F32, name="tg")
                 st[("tg", k)] = tg
             for i in range(4):
+                xcol, col = block_args(k, i)
                 if kind == 0:
                     u, vh, e = (k // 2) % 2, k // 4, k % 2
-                    xcol = 8 + u
-                    col = 16 * u + 8 * e + 4 * vh + i
                     dst = rs_all[:, 2 * u + e, 4 * vh + i, :]
                 else:
-                    xcol = s // 2 if kind == 1 else s
-                    col = 4 * s + i
                     dst = q_t[:, s, i, :] if kind == 1 else tg[:, i, :]
-                nc.vector.scalar_tensor_tensor(out=tmp[:, i, :], in0=xb[:, xcol, :], scalar=svf[:, 2 * kind, col:col + 1],
-                                               in1=acc[:, i, :], op0=ALU.mult, op1=ALU.add)
                 nc.scalar.activation(out=dst, in_=tmp[:, i, :], func=(ACTF.Tanh if kind == 2 else ACTF.Sigmoid),
                                      bias=svf[:, 2 * kind + 1, col:col + 1], scale=(-1.0 if kind == 1 else 1.0))
 
@@ -301,42 +298,50 @@ def tile_grucell_kernel(
         def n_on_pool(k):
             return (k % 8) < N_POOL_UPTO
 
+        def step_n(k):
+            return k + LAG_A if n_on_pool(k) else k + LAG_A + 1
+
         def step_b(k):
             if k < 16:
                 return k + LAG_BZ
-            return k + LAG_BG if n_on_pool(k) else k + LAG_M + 2
+            return k + LAG_BG if n_on_pool(k) else k + LAG_A + 2
 
-        for i in range(N_CHUNKS + 10):
+        for i in range(N_CHUNKS + 14):
             if i < N_CHUNKS:
                 do_t(i)
-            if i < LAG_M:
-                dummies(wbank, D_STEP0)
+            if 0 <= i - 1 < N_CHUNKS:
+                do_q(i - 1)
+            if i == 1:
+                do_xev()
+            if 0 <= i - LAG_M < N_CHUNKS:
+                do_m(i - LAG_M)
             for k in range(8, N_CHUNKS):
                 if step_b(k) == i:
                     do_b(k)
-            if 0 <= i - 1 < N_CHUNKS:
-                do_q(i - 1)
-            km = i - LAG_M
-            if 0 <= km < N_CHUNKS:
-                do_m(km)
-            if i == 6:
+            if i == 8:
                 nc.vector.tensor_copy(out=svf[:, 2, :], in_=sv[:, 2, :])
                 nc.vector.tensor_scalar_mul(out=svf[:, 3, :], in0=sv[:, 3, :], scalar1=-1.0)
                 nc.vector.tensor_copy(out=svf[:, 4:6, :], in_=sv[:, 4:6, :])
             for hh in range(2):
                 if i == QH_STEPS[hh]:
                     do_qh(hh)
-            if 16 <= km - 1 < N_CHUNKS and not n_on_pool(km - 1):
-                do_n(km - 1)
+            for k in range(16, N_CHUNKS):
+                if not n_on_pool(k) and step_n(k) == i:
+                    do_n(k)
             for k in range(8, N_CHUNKS):
                 if step_b(k) + 1 == i:
                     do_x(k)
             if i < N_CHUNKS:
                 do_c(i)
-            if 0 <= km < N_CHUNKS:
-                do_sa(km)
-                if km == 3 or km == 7:
-                    for v in range(km - 3, km + 1):
+            if i == 0:
+                do_h(0)
+            if 0 <= i - LAG_S < N_CHUNKS:
+                do_s(i - LAG_S)
+            ka = i - LAG_A
+            if 0 <= ka < N_CHUNKS:
+                do_a(ka)
+                if ka == 3 or ka == 7:
+                    for v in range(ka - 3, ka + 1):
                         do_hr(v)
-                if km >= 16 and n_on_pool(km):
-                    do_n(km)
+                if ka >= 16 and n_on_pool(ka):
+                    do_n(ka)

@@ -19,7 +19,7 @@ N_CHUNKS = 24
 MANUAL = True
 HR_POOL = True
 N_POOL_UPTO = 6
-DVE_EVAC = ((1, 1), (3, 1), (5, 1), (7, 1))
+DVE_EVAC = ((1, 1), (3, 1), (5, 1), (7, 1), (9, 1), (11, 1), (13, 1), (15, 1))
 RAW_BUFS = 16
 QH_STEPS = (13, 18)
 LAG_S = 2

@@ -18,15 +18,19 @@ N_CHUNKS = 24
 
 MANUAL = True
 HR_POOL = True
-N_POOL_UPTO = 6
-DVE_EVAC = ((1, 1), (3, 1), (5, 1), (7, 1), (9, 1), (11, 1), (13, 1), (15, 1))
-RAW_BUFS = 16
+N_POOL_UPTO = 7
+DVE_EVAC = ((1, 1), (3, 1), (5, 1), (7, 1))
+RAW_BUFS = 14
 QH_STEPS = (13, 18)
 LAG_S = 2
+SPLIT = 2
+Q_PAIR = False
+GRP_BUFS = 3
+W4_BUFS = 6
 LAG_A = 3
 LAG_M = 2
 LAG_BZ = 5
-LAG_BG = 6
+LAG_BG = 7
 N_RCODES = 3
 
 
@@ -42,10 +46,10 @@ def tile_grucell_kernel(
     with ExitStack() as ctx:
         const = ctx.enter_context(tc.tile_pool(name="const", bufs=1))
         rawp = ctx.enter_context(tc.tile_pool(name="rawp", bufs=RAW_BUFS))
-        grpp = ctx.enter_context(tc.tile_pool(name="grpp", bufs=3))
-        codp = ctx.enter_context(tc.tile_pool(name="codp", bufs=3))
+        grpp = ctx.enter_context(tc.tile_pool(name="grpp", bufs=GRP_BUFS))
+        codp = ctx.enter_context(tc.tile_pool(name="codp", bufs=GRP_BUFS))
         wrk = ctx.enter_context(tc.tile_pool(name="wrk", bufs=3))
-        wrk4 = ctx.enter_context(tc.tile_pool(name="wrk4", bufs=4))
+        wrk4 = ctx.enter_context(tc.tile_pool(name="wrk4", bufs=W4_BUFS))
         ps_w = ctx.enter_context(tc.psum_pool(name="ps_w", bufs=4))
         ps_a = ctx.enter_context(tc.psum_pool(name="ps_a", bufs=2))
         ps_b = ctx.enter_context(tc.psum_pool(name="ps_b", bufs=2))
@@ -259,8 +263,11 @@ def tile_grucell_kernel(
 
         def do_hr(v):
             eng = nc.gpsimd if HR_POOL else nc.vector
-            eng.tensor_tensor(out=hrg[:, v, :, :], in0=rs_all[:, :, v, :].rearrange("p t b -> p b t"),
-                              in1=hgb[:, v, :, :], op=ALU.mult)
+            w = P // SPLIT
+            for part in range(SPLIT):
+                bs = slice(w * part, w * part + w)
+                eng.tensor_tensor(out=hrg[:, v, bs, :], in0=rs_all[:, :, v, bs].rearrange("p t b -> p b t"),
+                                  in1=hgb[:, v, bs, :], op=ALU.mult)
 
         def do_qh(hh):
             nc.vector.quantize_mx(out=hrq[:, 512 * hh:512 * hh + 512].bitcast(FP8X4),
@@ -272,8 +279,13 @@ def tile_grucell_kernel(
             nt = wrk4.tile([P, 4, P], F32, name="nt")
             st[("nt", k)] = nt
             eng = nc.gpsimd if s < N_POOL_UPTO else nc.vector
-            eng.tensor_tensor(out=nt[:].rearrange("p n b -> p (n b)"), in0=q_t[:, s, :, :].rearrange("p n b -> p (n b)"),
-                              in1=st[("tg", k)][:].rearrange("p n b -> p (n b)"), op=ALU.mult)
+            parts = SPLIT if s < N_POOL_UPTO else 1
+            w = 4 // parts
+            for part in range(parts):
+                ns = slice(w * part, w * part + w)
+                eng.tensor_tensor(out=nt[:, ns, :].rearrange("p n b -> p (n b)"),
+                                  in0=q_t[:, s, ns, :].rearrange("p n b -> p (n b)"),
+                                  in1=st[("tg", k)][:, ns, :].rearrange("p n b -> p (n b)"), op=ALU.mult)
 
         def do_b(k):
             s = k % 8
@@ -306,11 +318,19 @@ def tile_grucell_kernel(
                 return k + LAG_BZ
             return k + LAG_BG if n_on_pool(k) else k + LAG_A + 2
 
-        for i in range(N_CHUNKS + 14):
+        for i in range(N_CHUNKS + 16):
             if i < N_CHUNKS:
                 do_t(i)
-            if 0 <= i - 1 < N_CHUNKS:
+            if Q_PAIR:
+                if i % 2 == 0:
+                    for k in (i - 2, i - 1):
+                        if 0 <= k < N_CHUNKS:
+                            do_q(k)
+            elif 0 <= i - 1 < N_CHUNKS:
                 do_q(i - 1)
+            for hh in range(2):
+                if i == QH_STEPS[hh]:
+                    do_qh(hh)
             if i == 1:
                 do_xev()
             if 0 <= i - LAG_M < N_CHUNKS:
@@ -322,9 +342,6 @@ def tile_grucell_kernel(
                 nc.vector.tensor_copy(out=svf[:, 2, :], in_=sv[:, 2, :])
                 nc.vector.tensor_scalar_mul(out=svf[:, 3, :], in0=sv[:, 3, :], scalar1=-1.0)
                 nc.vector.tensor_copy(out=svf[:, 4:6, :], in_=sv[:, 4:6, :])
-            for hh in range(2):
-                if i == QH_STEPS[hh]:
-                    do_qh(hh)
             for k in range(16, N_CHUNKS):
                 if not n_on_pool(k) and step_n(k) == i:
                     do_n(k)

@@ -21,16 +21,16 @@ HR_POOL = True
 N_POOL_UPTO = 7
 DVE_EVAC = ((1, 1), (3, 1), (5, 1), (7, 1))
 RAW_BUFS = 14
-QH_STEPS = (13, 18)
-LAG_S = 2
+QH_STEPS = (14, 19)
+LAG_S = 3
 SPLIT = 2
 Q_PAIR = False
 GRP_BUFS = 3
 W4_BUFS = 6
-LAG_A = 3
-LAG_M = 2
-LAG_BZ = 5
-LAG_BG = 7
+LAG_A = 4
+LAG_M = 3
+LAG_BZ = 6
+LAG_BG = 8
 N_RCODES = 3
 
 
@@ -189,12 +189,14 @@ def tile_grucell_kernel(
             grp = st[("grp", k)]
             if k < 8:
                 codes, scales = rcodes[k % N_RCODES], rscales[k % N_RCODES]
-                for i in range(4):
-                    for h in range(2):
-                        c0 = 192 * i + 128 * h
-                        nc.vector.quantize_mx(
-                            out=codes[:, c0:c0 + 64].bitcast(FP8X4), scales=scales[:, c0:c0 + 64],
-                            in_=grp[:, i, 64 * h:64 * h + 64, :].rearrange("p c u -> p (c u)").bitcast(BF16))
+                flat = grp[:].rearrange("p i c u -> p (i c u)").bitcast(BF16)
+                for first, last in ((0, 1), (1, 3), (3, 5), (5, 7), (7, 8)):
+                    i, h = first // 2, first % 2
+                    c0 = 192 * i + 128 * h
+                    w = 64 * (last - first)
+                    nc.vector.quantize_mx(
+                        out=codes[:, c0:c0 + w].bitcast(FP8X4), scales=scales[:, c0:c0 + w],
+                        in_=flat[:, 256 * first:256 * last])
             else:
                 codes = codp.tile([P, 512], U32, name="codes", align_bytes=64)
                 scales = codp.tile([P, 512], U8, name="scales", align_bytes=64)

@@ -20,18 +20,21 @@ MANUAL = True
 HR_POOL = True
 N_POOL_UPTO = 7
 DVE_EVAC = ((1, 1), (3, 1), (5, 1), (7, 1))
-RAW_BUFS = 14
-QH_STEPS = (14, 19)
+RAW_BUFS = 12
+QH_STEPS = (13, 18)
 LAG_S = 3
 SPLIT = 2
 Q_PAIR = False
-GRP_BUFS = 3
+GRP_BUFS = 4
 W4_BUFS = 6
 LAG_A = 4
 LAG_M = 3
 LAG_BZ = 6
-LAG_BG = 8
+LAG_BG = 6
 N_RCODES = 3
+XEV_STEP = 2
+H0_STEP = 1
+HC_V = (1, 3)
 
 
 def tile_grucell_kernel(
@@ -49,6 +52,7 @@ def tile_grucell_kernel(
         grpp = ctx.enter_context(tc.tile_pool(name="grpp", bufs=GRP_BUFS))
         codp = ctx.enter_context(tc.tile_pool(name="codp", bufs=GRP_BUFS))
         wrk = ctx.enter_context(tc.tile_pool(name="wrk", bufs=3))
+        outp = ctx.enter_context(tc.tile_pool(name="outp", bufs=6))
         wrk4 = ctx.enter_context(tc.tile_pool(name="wrk4", bufs=W4_BUFS))
         ps_w = ctx.enter_context(tc.psum_pool(name="ps_w", bufs=4))
         ps_a = ctx.enter_context(tc.psum_pool(name="ps_a", bufs=2))
@@ -149,7 +153,7 @@ def tile_grucell_kernel(
                     for uk in range(2):
                         nc.tensor.transpose(ht[:, vi, uk, :],
                                             hs[:, 2 * vp + vi, :].bitcast(F32)[:, 128 * uk:128 * uk + 128], ident_f[:])
-                eng_copy = nc.scalar.copy if vp % 2 == 0 else nc.vector.tensor_copy
+                eng_copy = nc.vector.tensor_copy if vp in HC_V else nc.scalar.copy
                 eng_copy(out=hgrp[:, 2 * vp:2 * vp + 2, :, :], in_=ht[:].rearrange("p v u b -> p v b u"))
             nc.vector.quantize_mx(out=hq[:, 512 * hh:512 * hh + 512].bitcast(FP8X4), scales=hqs[:, 512 * hh:512 * hh + 512],
                                   in_=hgrp[:, 4 * hh:4 * hh + 4, :, :].rearrange("p v b u -> p (v b u)").bitcast(BF16))
@@ -304,7 +308,7 @@ def tile_grucell_kernel(
                                                in1=hid[:, 512 * s:512 * s + 512].rearrange("b (p n) -> b p n", n=4),
                                                op0=ALU.subtract, op1=ALU.mult)
             else:
-                o_sb = wrk.tile([P, 512], F32, name="o_sb")
+                o_sb = outp.tile([P, 512], F32, name="o_sb")
                 nc.vector.tensor_tensor(out=o_sb[:].rearrange("b (p n) -> b p n", n=4), in0=bkv,
                                         in1=nega[:, s, :].rearrange("b (p n) -> b p n", n=4), op=ALU.subtract)
                 nc.sync.dma_start(out=out[:, 512 * s:512 * s + 512], in_=o_sb[:])
@@ -333,7 +337,7 @@ def tile_grucell_kernel(
             for hh in range(2):
                 if i == QH_STEPS[hh]:
                     do_qh(hh)
-            if i == 1:
+            if i == XEV_STEP:
                 do_xev()
             if 0 <= i - LAG_M < N_CHUNKS:
                 do_m(i - LAG_M)
@@ -352,7 +356,7 @@ def tile_grucell_kernel(
                     do_x(k)
             if i < N_CHUNKS:
                 do_c(i)
-            if i == 0:
+            if i == H0_STEP:
                 do_h(0)
             if 0 <= i - LAG_S < N_CHUNKS:
                 do_s(i - LAG_S)

@@ -21,7 +21,7 @@ HR_POOL = True
 N_POOL_UPTO = 7
 DVE_EVAC = ((1, 1), (3, 1), (5, 1), (7, 1))
 RAW_BUFS = 12
-QH_STEPS = (13, 18)
+QH_STEPS = (15, 20)
 LAG_S = 3
 SPLIT = 2
 Q_PAIR = False
@@ -30,9 +30,16 @@ W4_BUFS = 6
 LAG_A = 4
 LAG_M = 3
 LAG_BZ = 6
-LAG_BG = 6
+LAG_BG = 8
 N_RCODES = 3
 XEV_STEP = 2
+SV_AT = 2
+ROW_AT = 5
+V_STEP = 7
+SORT_V = (4, 8)
+SORT_S = (0, 2)
+SORT_G = (2, 4)
+UK = True
 H0_STEP = 1
 HC_V = (1, 3)
 
@@ -62,11 +69,9 @@ def tile_grucell_kernel(
 
         x_sb = const.tile([P, 8], BF16, name="x_sb")
         nc.scalar.dma_start(out=x_sb[:], in_=x_in)
-        sv = const.tile([P, 6, 32], BF16, name="sv")
-        nc.scalar.dma_start(out=sv[:, 0, :].rearrange("p (u n) -> p u n", u=2),
-                            in_=gwi[4096:8192].rearrange("(u p n) -> p u n", u=2, n=16))
-        nc.scalar.dma_start(out=sv[:, 1, :].rearrange("p (u n) -> p u n", u=2),
-                            in_=gate_bias[4096:8192].rearrange("(u p n) -> p u n", u=2, n=16))
+        sv = const.tile([P, 2, 32], BF16, name="sv")
+        vrow = const.tile([P, 512], BF16, name="vrow")
+        nc.vector.memset(vrow[:], 0.0)
 
         hid = const.tile([P, 4096], BF16, name="hid")
         for half in range(2):
@@ -86,10 +91,14 @@ def tile_grucell_kernel(
                 s = k % 8
                 nc.sync.dma_start(out=raw[:], in_=mat[512 * s:512 * s + 512, :].rearrange("(p n) j -> p n j", n=4))
             raws.append(raw)
-            if k == 5:
-                for idx, vecsrc in ((2, gwi[0:4096]), (3, gate_bias[0:4096]), (4, uwi), (5, update_bias)):
-                    nc.sync.dma_start(out=sv[:, idx, :].rearrange("p (s n) -> p s n", s=8),
-                                      in_=vecsrc.rearrange("(s p n) -> p s n", s=8, n=4))
+            if k == SV_AT:
+                nc.sync.dma_start(out=sv[:, 0, :].rearrange("p (u n) -> p u n", u=2),
+                                  in_=gwi[4096:8192].rearrange("(u p n) -> p u n", u=2, n=16))
+                nc.sync.dma_start(out=sv[:, 1, :].rearrange("p (u n) -> p u n", u=2),
+                                  in_=gate_bias[4096:8192].rearrange("(u p n) -> p u n", u=2, n=16))
+            if k == ROW_AT:
+                for idx, vecsrc in enumerate((gwi[0:4096], gate_bias[0:4096], uwi, update_bias)):
+                    nc.sync.dma_start(out=vrow[8 * idx:8 * idx + 8, :], in_=vecsrc.rearrange("(s x) -> s x", x=512))
 
         ident_b = const.tile([P, P], BF16, name="ident_b")
         make_identity(nc, ident_b[:])
@@ -111,37 +120,47 @@ def tile_grucell_kernel(
             rscales.append(rs_)
 
         xrep = const.tile([P, 4, 64], BF16, name="xrep")
-        nc.vector.tensor_copy(out=xrep[:], in_=x_sb[:, 4:8].unsqueeze(2).to_broadcast([P, 4, 64]))
         xb = const.tile([P, 10, P], F32, name="xb")
-        xp2 = ps_b.tile([P, 4, P], F32, name="bk")
-        for u in range(2):
-            nc.tensor.matmul(out=xp2[:, u, :], lhsT=xrep[:, 2 * u:2 * u + 2, :].rearrange("p a c -> p (a c)"),
-                             rhs=ident_b[:], start=True, stop=True)
-        xps = []
-        for g in range(2):
-            xp = ps_a.tile([P, 4, P], F32, name="acc")
-            for vi in range(4):
-                v = 4 * g + vi
-                nc.tensor.matmul(out=xp[:, vi, :], lhsT=x_sb[:, v:v + 1].to_broadcast([P, P]), rhs=ident_b[:],
-                                 start=True, stop=True)
-            xps.append(xp)
+        svf = const.tile([P, 6, 32], F32, name="svf")
+        negb = const.tile([P, 32], F32, name="negb")
+        st = {}
+
+        def do_x_pe():
+            xp2 = ps_b.tile([P, 4, P], F32, name="bk")
+            for u in range(2):
+                nc.tensor.matmul(out=xp2[:, u, :], lhsT=xrep[:, 2 * u:2 * u + 2, :].rearrange("p a c -> p (a c)"),
+                                 rhs=ident_b[:], start=True, stop=True)
+            st["xp2"] = xp2
+            for g in range(2):
+                xp = ps_a.tile([P, 4, P], F32, name="acc")
+                for vi in range(4):
+                    v = 4 * g + vi
+                    nc.tensor.matmul(out=xp[:, vi, :], lhsT=x_sb[:, v:v + 1].to_broadcast([P, P]), rhs=ident_b[:],
+                                     start=True, stop=True)
+                st[("xp", g)] = xp
 
         def do_xev():
-            nc.scalar.copy(out=xb[:, 8:10, :], in_=xp2[:, 0:2, :])
+            nc.scalar.copy(out=xb[:, 8:10, :], in_=st["xp2"][:, 0:2, :])
             for g in range(2):
-                nc.scalar.copy(out=xb[:, 4 * g:4 * g + 4, :], in_=xps[g][:])
+                nc.scalar.copy(out=xb[:, 4 * g:4 * g + 4, :], in_=st[("xp", g)][:])
 
-        svf = const.tile([P, 6, 32], F32, name="svf")
-        nc.vector.tensor_copy(out=svf[:, 0:2, :], in_=sv[:, 0:2, :])
+        def do_v():
+            vt = ps_b.tile([P, 4, P], BF16, name="bk")
+            st["vt"] = vt
+            for n in range(4):
+                nc.tensor.transpose(vt[:, n, :], vrow[:].rearrange("p (c n) -> p n c", n=4)[:, n, :], ident_b[:])
+
+        nc.vector.tensor_copy(out=xrep[:], in_=x_sb[:, 4:8].unsqueeze(2).to_broadcast([P, 4, 64]))
+        do_x_pe()
 
         hs = const.tile([P, 8, 512], BF16, name="hs")
         for half in range(2):
             src = hid[:, 2048 * half:2048 * half + 2048].rearrange("b (j v) -> b v j", v=8)
             cols = slice(256 * half, 256 * half + 256)
-            nc.vector.tensor_copy(out=hs[:, 0:4, cols], in_=src[:, 0:4, :])
-            nc.scalar.copy(out=hs[:, 4:6, cols], in_=src[:, 4:6, :])
-            nc.gpsimd.tensor_scalar(out=hs[:, 6:8, cols], in0=src[:, 6:8, :], scalar1=1.0, scalar2=0.0,
-                                    op0=ALU.mult, op1=ALU.add)
+            nc.vector.tensor_copy(out=hs[:, SORT_V[0]:SORT_V[1], cols], in_=src[:, SORT_V[0]:SORT_V[1], :])
+            nc.scalar.copy(out=hs[:, SORT_S[0]:SORT_S[1], cols], in_=src[:, SORT_S[0]:SORT_S[1], :])
+            nc.gpsimd.tensor_scalar(out=hs[:, SORT_G[0]:SORT_G[1], cols], in0=src[:, SORT_G[0]:SORT_G[1], :], scalar1=1.0,
+                                    scalar2=0.0, op0=ALU.mult, op1=ALU.add)
         hgrp = const.tile([P, 8, P, 2], F32, name="hgrp", align_bytes=64)
         hq = const.tile([P, 1024], U32, name="hq", align_bytes=64)
         hqs = const.tile([P, 1024], U8, name="hqs", align_bytes=64)
@@ -149,8 +168,7 @@ def tile_grucell_kernel(
         def do_h(hh):
             for vp in (2 * hh, 2 * hh + 1):
                 ht = ps_w.tile([P, 2, 2, P], F32, name="wt")
-                for vi in range(2):
-                    for uk in range(2):
+                for vi, uk in (((0, 0), (1, 0), (0, 1), (1, 1)) if UK else ((0, 0), (0, 1), (1, 0), (1, 1))):
                         nc.tensor.transpose(ht[:, vi, uk, :],
                                             hs[:, 2 * vp + vi, :].bitcast(F32)[:, 128 * uk:128 * uk + 128], ident_f[:])
                 eng_copy = nc.vector.tensor_copy if vp in HC_V else nc.scalar.copy
@@ -167,8 +185,6 @@ def tile_grucell_kernel(
         hrg = const.tile([P, 8, P, 4], BF16, name="hrg", align_bytes=64)
         hrq = const.tile([P, 1024], U32, name="hrq", align_bytes=64)
         hrqs = const.tile([P, 1024], U8, name="hrqs", align_bytes=64)
-
-        st = {}
 
         def do_t(k):
             raw = raws[k]
@@ -265,7 +281,7 @@ def tile_grucell_kernel(
                 else:
                     dst = q_t[:, s, i, :] if kind == 1 else tg[:, i, :]
                 nc.scalar.activation(out=dst, in_=tmp[:, i, :], func=(ACTF.Tanh if kind == 2 else ACTF.Sigmoid),
-                                     bias=svf[:, 2 * kind + 1, col:col + 1], scale=(-1.0 if kind == 1 else 1.0))
+                                     bias=(negb[:, col:col + 1] if kind == 1 else svf[:, 2 * kind + 1, col:col + 1]), scale=(-1.0 if kind == 1 else 1.0))
 
         def do_hr(v):
             eng = nc.gpsimd if HR_POOL else nc.vector
@@ -344,10 +360,15 @@ def tile_grucell_kernel(
             for k in range(8, N_CHUNKS):
                 if step_b(k) == i:
                     do_b(k)
-            if i == 8:
-                nc.vector.tensor_copy(out=svf[:, 2, :], in_=sv[:, 2, :])
-                nc.vector.tensor_scalar_mul(out=svf[:, 3, :], in0=sv[:, 3, :], scalar1=-1.0)
-                nc.vector.tensor_copy(out=svf[:, 4:6, :], in_=sv[:, 4:6, :])
+            if i == V_STEP:
+                do_v()
+            if i == V_STEP + 1:
+                nc.vector.tensor_copy(out=svf[:, 2:6, :].rearrange("p a (s n) -> p (a s) n", n=4),
+                                      in_=st["vt"][:, :, 0:32].rearrange("p n r -> p r n"))
+            if i == V_STEP + 2:
+                nc.vector.tensor_scalar_mul(out=negb[:], in0=svf[:, 3, :], scalar1=-1.0)
+            if i == LAG_S:
+                nc.vector.tensor_copy(out=svf[:, 0:2, :], in_=sv[:])
             for k in range(16, N_CHUNKS):
                 if not n_on_pool(k) and step_n(k) == i:
                     do_n(k)

from contextlib import ExitStack

import concourse.mybir as mybir
from concourse.masks import make_identity

F32 = mybir.dt.float32
BF16 = mybir.dt.bfloat16
U32 = mybir.dt.uint32
U8 = mybir.dt.uint8
I32 = mybir.dt.int32
FP8X4 = mybir.dt.float8_e4m3fn_x4
ALU = mybir.AluOpType
ACTF = mybir.ActivationFunctionType

P = 128
FLOPS = 2 * 128 * 512 * (8192 + 4096)
N_CHUNKS = 24

MANUAL = True
HR_POOL = True
N_POOL_UPTO = 7
DVE_EVAC = ((1, 1), (3, 1), (5, 1), (7, 1))
RAW_BUFS = 12
QH_STEPS = (15, 20)
LAG_S = 3
SPLIT = 2
Q_PAIR = False
GRP_BUFS = 4
W4_BUFS = 6
LAG_A = 4
LAG_M = 3
LAG_BZ = 6
LAG_BG = 8
N_RCODES = 3
XEV_STEP = 2
SV_AT = 2
ROW_AT = 5
V_STEP = 7
SORT_V = (4, 8)
SORT_S = (0, 2)
SORT_G = (2, 4)
UK = True
H0_STEP = 1
HC_V = (1, 3)


def tile_grucell_kernel(
    tc, x_in, hidden, gate_w_i2h, gate_w_h2h, gate_bias, update_w_i2h, update_w_h2h, update_bias, out
):
    nc = tc.nc
    gw = gate_w_h2h.rearrange("v o c j -> (v o c) j")
    uw = update_w_h2h.rearrange("v o c j -> (v o c) j")
    gwi = gate_w_i2h.rearrange("v o c i -> (v o c i)")
    uwi = update_w_i2h.rearrange("v o c i -> (v o c i)")

    with ExitStack() as ctx:
        const = ctx.enter_context(tc.tile_pool(name="const", bufs=1))
        rawp = ctx.enter_context(tc.tile_pool(name="rawp", bufs=RAW_BUFS))
        grpp = ctx.enter_context(tc.tile_pool(name="grpp", bufs=GRP_BUFS))
        codp = ctx.enter_context(tc.tile_pool(name="codp", bufs=GRP_BUFS))
        wrk = ctx.enter_context(tc.tile_pool(name="wrk", bufs=3))
        outp = ctx.enter_context(tc.tile_pool(name="outp", bufs=6))
        wrk4 = ctx.enter_context(tc.tile_pool(name="wrk4", bufs=W4_BUFS))
        ps_w = ctx.enter_context(tc.psum_pool(name="ps_w", bufs=4))
        ps_a = ctx.enter_context(tc.psum_pool(name="ps_a", bufs=2))
        ps_b = ctx.enter_context(tc.psum_pool(name="ps_b", bufs=2))
        if MANUAL:
            ctx.enter_context(tc.manual_schedule())

        x_sb = const.tile([P, 8], BF16, name="x_sb")
        nc.scalar.dma_start(out=x_sb[:], in_=x_in)
        sv = const.tile([P, 2, 32], BF16, name="sv")
        vrow = const.tile([P, 512], BF16, name="vrow")
        nc.vector.memset(vrow[:], 0.0)

        hid = const.tile([P, 4096], BF16, name="hid")
        for half in range(2):
            nc.sync.dma_start(out=hid[:, 2048 * half:2048 * half + 2048],
                              in_=hidden[:, 2048 * half:2048 * half + 2048])

        raws = []
        for k in range(N_CHUNKS):
            raw = rawp.tile([P, 4, 512], BF16, name="raw")
            if k < 8:
                u, vh, e = (k // 2) % 2, k // 4, k % 2
                src = gw[4096 + 2048 * u:4096 + 2048 * u + 2048, :].rearrange(
                    "(p e w i) j -> p e w i j", e=2, w=2, i=4)
                nc.sync.dma_start(out=raw[:], in_=src[:, e, vh, :, :])
            else:
                mat = gw if k < 16 else uw
                s = k % 8
                nc.sync.dma_start(out=raw[:], in_=mat[512 * s:512 * s + 512, :].rearrange("(p n) j -> p n j", n=4))
            raws.append(raw)
            if k == SV_AT:
                nc.sync.dma_start(out=sv[:, 0, :].rearrange("p (u n) -> p u n", u=2),
                                  in_=gwi[4096:8192].rearrange("(u p n) -> p u n", u=2, n=16))
                nc.sync.dma_start(out=sv[:, 1, :].rearrange("p (u n) -> p u n", u=2),
                                  in_=gate_bias[4096:8192].rearrange("(u p n) -> p u n", u=2, n=16))
            if k == ROW_AT:
                for idx, vecsrc in enumerate((gwi[0:4096], gate_bias[0:4096], uwi, update_bias)):
                    nc.sync.dma_start(out=vrow[8 * idx:8 * idx + 8, :], in_=vecsrc.rearrange("(s x) -> s x", x=512))

        ident_b = const.tile([P, P], BF16, name="ident_b")
        make_identity(nc, ident_b[:])
        ident_f = const.tile([P, P], F32, name="ident_f")
        make_identity(nc, ident_f[:])

        warm = const.tile([P, 1], F32, name="warm")
        nc.vector.memset(warm[:], 0.0)
        nc.scalar.activation(out=warm[:], in_=warm[:], func=ACTF.Sigmoid)

        rcodes = []
        rscales = []
        for i in range(N_RCODES):
            rc = const.tile([P, 768], U32, name="rcodes%d" % i, align_bytes=64)
            rs_ = const.tile([P, 768], U8, name="rscales%d" % i, align_bytes=64)
            nc.vector.memset(rc[:].bitcast(I32), 0)
            nc.vector.memset(rs_[:].bitcast(I32), 0)
            rcodes.append(rc)
            rscales.append(rs_)

        xrep = const.tile([P, 4, 64], BF16, name="xrep")
        xb = const.tile([P, 10, P], F32, name="xb")
        svf = const.tile([P, 6, 32], F32, name="svf")
        negb = const.tile([P, 32], F32, name="negb")
        st = {}

        def do_x_pe():
            xp2 = ps_b.tile([P, 4, P], F32, name="bk")
            for u in range(2):
                nc.tensor.matmul(out=xp2[:, u, :], lhsT=xrep[:, 2 * u:2 * u + 2, :].rearrange("p a c -> p (a c)"),
                                 rhs=ident_b[:], start=True, stop=True)
            st["xp2"] = xp2
            for g in range(2):
                xp = ps_a.tile([P, 4, P], F32, name="acc")
                for vi in range(4):
                    v = 4 * g + vi
                    nc.tensor.matmul(out=xp[:, vi, :], lhsT=x_sb[:, v:v + 1].to_broadcast([P, P]), rhs=ident_b[:],
                                     start=True, stop=True)
                st[("xp", g)] = xp

        def do_xev():
            nc.scalar.copy(out=xb[:, 8:10, :], in_=st["xp2"][:, 0:2, :])
            for g in range(2):
                nc.scalar.copy(out=xb[:, 4 * g:4 * g + 4, :], in_=st[("xp", g)][:])

        def do_v():
            vt = ps_b.tile([P, 4, P], BF16, name="bk")
            st["vt"] = vt
            for n in range(4):
                nc.tensor.transpose(vt[:, n, :], vrow[:].rearrange("p (c n) -> p n c", n=4)[:, n, :], ident_b[:])

        nc.vector.tensor_copy(out=xrep[:], in_=x_sb[:, 4:8].unsqueeze(2).to_broadcast([P, 4, 64]))
        do_x_pe()

        hs = const.tile([P, 8, 512], BF16, name="hs")
        for half in range(2):
            src = hid[:, 2048 * half:2048 * half + 2048].rearrange("b (j v) -> b v j", v=8)
            cols = slice(256 * half, 256 * half + 256)
            nc.vector.tensor_copy(out=hs[:, SORT_V[0]:SORT_V[1], cols], in_=src[:, SORT_V[0]:SORT_V[1], :])
            nc.scalar.copy(out=hs[:, SORT_S[0]:SORT_S[1], cols], in_=src[:, SORT_S[0]:SORT_S[1], :])
            nc.gpsimd.tensor_scalar(out=hs[:, SORT_G[0]:SORT_G[1], cols], in0=src[:, SORT_G[0]:SORT_G[1], :], scalar1=1.0,
                                    scalar2=0.0, op0=ALU.mult, op1=ALU.add)
        hgrp = const.tile([P, 8, P, 2], F32, name="hgrp", align_bytes=64)
        hq = const.tile([P, 1024], U32, name="hq", align_bytes=64)
        hqs = const.tile([P, 1024], U8, name="hqs", align_bytes=64)

        def do_h(hh):
            for vp in (2 * hh, 2 * hh + 1):
                ht = ps_w.tile([P, 2, 2, P], F32, name="wt")
                for vi, uk in (((0, 0), (1, 0), (0, 1), (1, 1)) if UK else ((0, 0), (0, 1), (1, 0), (1, 1))):
                        nc.tensor.transpose(ht[:, vi, uk, :],
                                            hs[:, 2 * vp + vi, :].bitcast(F32)[:, 128 * uk:128 * uk + 128], ident_f[:])
                eng_copy = nc.vector.tensor_copy if vp in HC_V else nc.scalar.copy
                eng_copy(out=hgrp[:, 2 * vp:2 * vp + 2, :, :], in_=ht[:].rearrange("p v u b -> p v b u"))
            nc.vector.quantize_mx(out=hq[:, 512 * hh:512 * hh + 512].bitcast(FP8X4), scales=hqs[:, 512 * hh:512 * hh + 512],
                                  in_=hgrp[:, 4 * hh:4 * hh + 4, :, :].rearrange("p v b u -> p (v b u)").bitcast(BF16))

        do_h(1)
        hgb = hgrp[:].rearrange("p v b u -> p v (b u)").bitcast(BF16).rearrange("p v (b t) -> p v b t", t=4)

        rs_all = const.tile([P, 4, 8, P], F32, name="rs_all")
        q_t = const.tile([P, 8, 4, P], F32, name="q_t")
        nega = const.tile([P, 8, 512], F32, name="nega")
        hrg = const.tile([P, 8, P, 4], BF16, name="hrg", align_bytes=64)
        hrq = const.tile([P, 1024], U32, name="hrq", align_bytes=64)
        hrqs = const.tile([P, 1024], U8, name="hrqs", align_bytes=64)

        def do_t(k):
            raw = raws[k]
            for hb in range(2):
                wt = ps_w.tile([P, 2, 2, P], F32, name="wt")
                for bi in range(2):
                    for uk in range(2):
                        nc.tensor.transpose(
                            wt[:, bi, uk, :],
                            raw[:, 2 * hb + bi, :].bitcast(F32)[:, 128 * uk:128 * uk + 128],
                            ident_f[:])
                st[("wt", k, hb)] = wt

        def do_c(k):
            grp = grpp.tile([P, 4, P, 2], F32, name="grp", align_bytes=64)
            st[("grp", k)] = grp
            for hb in range(2):
                eng_copy = nc.vector.tensor_copy if (k, hb) in DVE_EVAC else nc.scalar.copy
                eng_copy(out=grp[:, 2 * hb:2 * hb + 2, :, :], in_=st[("wt", k, hb)][:].rearrange("p i u c -> p i c u"))

        def do_q(k):
            grp = st[("grp", k)]
            if k < 8:
                codes, scales = rcodes[k % N_RCODES], rscales[k % N_RCODES]
                flat = grp[:].rearrange("p i c u -> p (i c u)").bitcast(BF16)
                for first, last in ((0, 1), (1, 3), (3, 5), (5, 7), (7, 8)):
                    i, h = first // 2, first % 2
                    c0 = 192 * i + 128 * h
                    w = 64 * (last - first)
                    nc.vector.quantize_mx(
                        out=codes[:, c0:c0 + w].bitcast(FP8X4), scales=scales[:, c0:c0 + w],
                        in_=flat[:, 256 * first:256 * last])
            else:
                codes = codp.tile([P, 512], U32, name="codes", align_bytes=64)
                scales = codp.tile([P, 512], U8, name="scales", align_bytes=64)
                nc.vector.quantize_mx(out=codes[:].bitcast(FP8X4), scales=scales[:],
                                      in_=grp[:].rearrange("p i c u -> p (i c u)").bitcast(BF16))
            st[("codes", k)] = (codes, scales)

        def do_m(k):
            codes, scales = st[("codes", k)]
            acc = ps_a.tile([P, 4, P], F32, name="acc")
            st[("acc", k)] = acc
            s = k % 8
            if k < 8:
                u = (k // 2) % 2
                for i in range(4):
                    for h in range(2):
                        c0 = 192 * i + 64 * h
                        v = 4 + 2 * u + h
                        nc.tensor.matmul_mx(
                            out=acc[:, i, :],
                            lhsT=codes[:, c0:c0 + 128].bitcast(FP8X4), lhsT_scale=scales[:, c0:c0 + 128],
                            rhs=hq[:, 128 * v:128 * v + 128].bitcast(FP8X4), rhs_scale=hqs[:, 128 * v:128 * v + 128],
                            start=(h == 0), stop=(h == 1))
            else:
                v = s // 2 if k < 16 else s
                mov, movs = (hq, hqs) if k < 16 else (hrq, hrqs)
                for i in range(4):
                    nc.tensor.matmul_mx(
                        out=acc[:, i, :],
                        lhsT=codes[:, 128 * i:128 * i + 128].bitcast(FP8X4), lhsT_scale=scales[:, 128 * i:128 * i + 128],
                        rhs=mov[:, 128 * v:128 * v + 128].bitcast(FP8X4), rhs_scale=movs[:, 128 * v:128 * v + 128],
                        start=True, stop=True)

        def block_args(k, i):
            kind, s = k // 8, k % 8
            if kind == 0:
                u, vh, e = (k // 2) % 2, k // 4, k % 2
                return 8 + u, 16 * u + 8 * e + 4 * vh + i
            return (s // 2 if kind == 1 else s), 4 * s + i

        def do_s(k):
            acc = st[("acc", k)]
            tmp = wrk.tile([P, 4, P], F32, name="tmp")
            st[("tmp", k)] = tmp
            for i in range(4):
                xcol, col = block_args(k, i)
                nc.vector.scalar_tensor_tensor(out=tmp[:, i, :], in0=xb[:, xcol, :],
                                               scalar=svf[:, 2 * (k // 8), col:col + 1],
                                               in1=acc[:, i, :], op0=ALU.mult, op1=ALU.add)

        def do_a(k):
            kind, s = k // 8, k % 8
            tmp = st[("tmp", k)]
            if kind == 2:
                tg = wrk4.tile([P, 4, P], F32, name="tg")
                st[("tg", k)] = tg
            for i in range(4):
                xcol, col = block_args(k, i)
                if kind == 0:
                    u, vh, e = (k // 2) % 2, k // 4, k % 2
                    dst = rs_all[:, 2 * u + e, 4 * vh + i, :]
                else:
                    dst = q_t[:, s, i, :] if kind == 1 else tg[:, i, :]
                nc.scalar.activation(out=dst, in_=tmp[:, i, :], func=(ACTF.Tanh if kind == 2 else ACTF.Sigmoid),
                                     bias=(negb[:, col:col + 1] if kind == 1 else svf[:, 2 * kind + 1, col:col + 1]), scale=(-1.0 if kind == 1 else 1.0))

        def do_hr(v):
            eng = nc.gpsimd if HR_POOL else nc.vector
            w = P // SPLIT
            for part in range(SPLIT):
                bs = slice(w * part, w * part + w)
                eng.tensor_tensor(out=hrg[:, v, bs, :], in0=rs_all[:, :, v, bs].rearrange("p t b -> p b t"),
                                  in1=hgb[:, v, bs, :], op=ALU.mult)

        def do_qh(hh):
            nc.vector.quantize_mx(out=hrq[:, 512 * hh:512 * hh + 512].bitcast(FP8X4),
                                  scales=hrqs[:, 512 * hh:512 * hh + 512],
                                  in_=hrg[:, 4 * hh:4 * hh + 4, :, :].rearrange("p v b t -> p (v b t)"))

        def do_n(k):
            s = k % 8
            nt = wrk4.tile([P, 4, P], F32, name="nt")
            st[("nt", k)] = nt
            eng = nc.gpsimd if s < N_POOL_UPTO else nc.vector
            parts = SPLIT if s < N_POOL_UPTO else 1
            w = 4 // parts
            for part in range(parts):
                ns = slice(w * part, w * part + w)
                eng.tensor_tensor(out=nt[:, ns, :].rearrange("p n b -> p (n b)"),
                                  in0=q_t[:, s, ns, :].rearrange("p n b -> p (n b)"),
                                  in1=st[("tg", k)][:, ns, :].rearrange("p n b -> p (n b)"), op=ALU.mult)

        def do_b(k):
            s = k % 8
            bk = ps_b.tile([P, 4, P], F32, name="bk")
            st[("bk", k)] = bk
            for i in range(4):
                nc.tensor.transpose(bk[:, i, :], q_t[:, s, i, :] if k < 16 else st[("nt", k)][:, i, :], ident_f[:])

        def do_x(k):
            s = k % 8
            bkv = st[("bk", k)][:].rearrange("b n p -> b p n")
            if k < 16:
                nc.vector.scalar_tensor_tensor(out=nega[:, s, :].rearrange("b (p n) -> b p n", n=4), in0=bkv, scalar=1.0,
                                               in1=hid[:, 512 * s:512 * s + 512].rearrange("b (p n) -> b p n", n=4),
                                               op0=ALU.subtract, op1=ALU.mult)
            else:
                o_sb = outp.tile([P, 512], F32, name="o_sb")
                nc.vector.tensor_tensor(out=o_sb[:].rearrange("b (p n) -> b p n", n=4), in0=bkv,
                                        in1=nega[:, s, :].rearrange("b (p n) -> b p n", n=4), op=ALU.subtract)
                nc.sync.dma_start(out=out[:, 512 * s:512 * s + 512], in_=o_sb[:])

        def n_on_pool(k):
            return (k % 8) < N_POOL_UPTO

        def step_n(k):
            return k + LAG_A if n_on_pool(k) else k + LAG_A + 1

        def step_b(k):
            if k < 16:
                return k + LAG_BZ
            return k + LAG_BG if n_on_pool(k) else k + LAG_A + 2

        for i in range(N_CHUNKS + 16):
            if i < N_CHUNKS:
                do_t(i)
            if Q_PAIR:
                if i % 2 == 0:
                    for k in (i - 2, i - 1):
                        if 0 <= k < N_CHUNKS:
                            do_q(k)
            elif 0 <= i - 1 < N_CHUNKS:
                do_q(i - 1)
            for hh in range(2):
                if i == QH_STEPS[hh]:
                    do_qh(hh)
            if i == XEV_STEP:
                do_xev()
            if 0 <= i - LAG_M < N_CHUNKS:
                do_m(i - LAG_M)
            for k in range(8, N_CHUNKS):
                if step_b(k) == i:
                    do_b(k)
            if i == V_STEP:
                do_v()
            if i == V_STEP + 1:
                nc.vector.tensor_copy(out=svf[:, 2:6, :].rearrange("p a (s n) -> p (a s) n", n=4),
                                      in_=st["vt"][:, :, 0:32].rearrange("p n r -> p r n"))
            if i == V_STEP + 2:
                nc.vector.tensor_scalar_mul(out=negb[:], in0=svf[:, 3, :], scalar1=-1.0)
            if i == LAG_S:
                nc.vector.tensor_copy(out=svf[:, 0:2, :], in_=sv[:])
            for k in range(16, N_CHUNKS):
                if not n_on_pool(k) and step_n(k) == i:
                    do_n(k)
            for k in range(8, N_CHUNKS):
                if step_b(k) + 1 == i:
                    do_x(k)
            if i < N_CHUNKS:
                do_c(i)
            if i == H0_STEP:
                do_h(0)
            if 0 <= i - LAG_S < N_CHUNKS:
                do_s(i - LAG_S)
            ka = i - LAG_A
            if 0 <= ka < N_CHUNKS:
                do_a(ka)
                if ka == 3 or ka == 7:
                    for v in range(ka - 3, ka + 1):
                        do_hr(v)
                if ka >= 16 and n_on_pool(ka):
                    do_n(ka)
